import numpy as np
import ml_dtypes


def mxq(x, axis, fmt="e4m3"):
    dtype, down = {"e4m3": (ml_dtypes.float8_e4m3fn, 7), "e5m2": (ml_dtypes.float8_e5m2, 14)}[fmt]
    v = np.moveaxis(np.asarray(x, np.float32).astype(ml_dtypes.bfloat16).astype(np.float64), axis, -1)
    blocks = v.reshape(v.shape[:-1] + (-1, 32))
    amax = np.abs(blocks).max(-1, keepdims=True)
    byte = np.maximum(np.where(amax > 0, np.frexp(amax)[1] - 1 + 127, 0) - down, 1)
    scale = np.exp2(byte - 127.0)
    codes = (blocks / scale).astype(np.float32).astype(dtype).astype(np.float64)
    return np.moveaxis((codes * scale).reshape(v.shape), -1, axis)


WIDE = False


def mx_kscale(k):
    if not WIDE:
        return np.ones(k)
    levels = np.array([10, -10, 5, -5, 0])
    a = np.random.permutation(np.resize(levels, k // 512 * 4)).reshape(k // 512, 4)
    idx = np.arange(k)
    return np.exp2(a[idx // 512, idx % 128 // 32])


BF16 = ml_dtypes.bfloat16


def bf(x):
    return np.asarray(x, np.float32).astype(BF16)


def f64(x):
    return np.asarray(x).astype(np.float64)


E2M1 = np.array([0.0, 0.5, 1.0, 1.5, 2.0, 3.0, 4.0, 6.0, -0.0, -0.5, -1.0, -1.5, -2.0, -3.0, -4.0, -6.0])


def pack_weight(w, fmt):
    k, n = w.shape
    w = f64(bf(w)).reshape(k // 32, 32, n)
    amax = np.abs(w).max(1)
    if fmt == "e4m3":
        byte = np.frexp(amax)[1] - 1 + 127 - 7
    else:
        mant, ex = np.frexp(amax / 6.0)
        byte = np.where(mant > 0.5, ex, ex - 1) + 127
    byte = np.clip(np.where(amax > 0, byte, 1), 1, 254)
    scaled = (w * np.exp2(127.0 - byte)[:, None, :]).reshape(k, n).astype(np.float32)
    by_word = np.ascontiguousarray(scaled.reshape(k // 512, 128, 4, n).transpose(0, 1, 3, 2))
    if fmt == "e4m3":
        words = by_word.astype(ml_dtypes.float8_e4m3fn).view(np.uint8)
    else:
        c = by_word.astype(ml_dtypes.float4_e2m1fn).view(np.uint8) & 0xF
        words = c[..., 0::2] | (c[..., 1::2] << 4)
    return np.ascontiguousarray(words), np.ascontiguousarray(byte.astype(np.uint8).reshape(k // 512, 16, n))


def unpack_weight(words, scales, fmt):
    g, p, n, _ = words.shape
    if fmt == "e4m3":
        vals = np.ascontiguousarray(words).view(ml_dtypes.float8_e4m3fn).astype(np.float64)
    else:
        nib = np.empty((g, p, n, 4), np.uint8)
        nib[..., 0::2] = words & 0xF
        nib[..., 1::2] = words >> 4
        vals = E2M1[nib]
    vals = vals * np.repeat(np.exp2(scales.astype(np.float64) - 127.0), 8, axis=1)[..., None]
    return vals.transpose(0, 1, 3, 2).reshape(g * 512, n)


B, S, D, O, G, P = 2, 512, 512, 512, 3, 3
NB = G + P


def silu(v):
    return v / (1.0 + np.exp(-v))


def extended_grid(d):
    pts = np.linspace(-1.0, 1.0, G + 1)
    h = 2.0 / G
    left = pts[0] + h * np.arange(-P, 0)
    right = pts[-1] + h * np.arange(1, P + 1)
    ext = np.concatenate([left, pts, right])
    return np.broadcast_to(ext, (d, ext.shape[0]))


def bspline_basis(x, grid):
    x = x[:, :, None]
    g = grid[None, :, :]
    bb = ((x >= g[..., :-1]) & (x < g[..., 1:])).astype(np.float64)
    for p in range(1, P + 1):
        left = (x - g[..., :-(p + 1)]) / (g[..., p:-1] - g[..., :-(p + 1)])
        right = (g[..., p + 1:] - x) / (g[..., p + 1:] - g[..., 1:-p])
        bb = left * bb[..., :-1] + right * bb[..., 1:]
    return bb


def setup_inputs():
    s = mx_kscale(D)
    u = s / s.max()
    x = bf(np.random.standard_normal((B, S, D)) * u)
    coef = bf(np.random.standard_normal((O, D, NB)) * 2.0 / np.sqrt(D))
    scale_base = (0.25 + (np.random.uniform(size=(O, D)) * 2.0 - 1.0) * 2.0) / np.sqrt(D) / u
    words, scales = pack_weight(np.ascontiguousarray(scale_base.T), "e4m3")
    scale_sp = bf(1.0 + 0.1 * np.random.standard_normal((O, D)))
    bias = bf(0.1 * np.random.standard_normal(O))
    return {"x": x,
            "coef": coef,
            "scale_base_words": words,
            "scale_base_scales": scales,
            "scale_sp": scale_sp,
            "bias": bias}


def reference(x, coef, scale_base_words, scale_base_scales, scale_sp, bias):
    x = f64(x)
    b_, s_, d = x.shape
    xf = x.reshape(-1, d)
    grid = extended_grid(d)
    basis = bspline_basis(xf, grid)
    base = silu(xf)
    spline_w = f64(scale_sp)[..., None] * f64(coef)
    y_base = mxq(base, 1, "e4m3") @ unpack_weight(scale_base_words, scale_base_scales, "e4m3")
    bt = np.ascontiguousarray(basis.transpose(2, 0, 1))
    wt = np.ascontiguousarray(spline_w.transpose(2, 1, 0))
    y_sp = (mxq(bt, 2, "e4m3") @ mxq(wt, 1, "e4m3")).sum(0)
    y = y_base + y_sp + f64(bias)[None, :]
    return y.reshape(b_, s_, -1)

@@ -1,0 +1,265 @@
+from contextlib import ExitStack
+
+import concourse.mybir as mybir
+from concourse.masks import make_identity
+
+F32 = mybir.dt.float32
+BF16 = mybir.dt.bfloat16
+U32 = mybir.dt.uint32
+U8 = mybir.dt.uint8
+I32 = mybir.dt.int32
+FP8X4 = mybir.dt.float8_e4m3fn_x4
+ALU = mybir.AluOpType
+ACT = mybir.ActivationFunctionType
+
+P = 128
+PACK = 4
+TOKENS = 1024
+FEATURES = 512
+OUTPUTS = 512
+NB = 6
+CHUNK_TOKENS = 256
+CHUNK = CHUNK_TOKENS * PACK
+CHUNKS = TOKENS // CHUNK_TOKENS
+MADE_IN_ORDER = (0, 4, 2, 1, 5, 3)
+TAIL_SCALE = 6.0 ** -0.5
+
+FLOPS = 2 * TOKENS * FEATURES * OUTPUTS * (NB + 1)
+
+
+def features_to_partitions(nc, psum, rows, ident, turned):
+    bank = psum.tile([P, 2, 2 * P], F32, tag="bank")
+    for a in range(2):
+        words = rows[:, a, :].bitcast(F32)
+        for h in range(2):
+            nc.tensor.transpose(bank[:, h, a * P : (a + 1) * P], words[:, h::2], ident)
+    nc.vector.tensor_copy(
+        out=turned.bitcast(F32).rearrange("p (r h) -> p r h", h=2),
+        in_=bank.rearrange("p h r -> p r h"),
+    )
+
+
+def tile_kanoriginal_kernel(
+    tc, x, coef, scale_base_words, scale_base_scales, scale_sp, bias, out
+):
+    nc = tc.nc
+    x_rows = x.flatten_outer_dims()
+    out_rows = out.flatten_outer_dims()
+
+    with ExitStack() as ctx:
+        keep = ctx.enter_context(tc.tile_pool(name="keep", bufs=1))
+        dist = ctx.enter_context(tc.tile_pool(name="dist", bufs=2))
+        squares = ctx.enter_context(tc.tile_pool(name="squares", bufs=4))
+        halves = ctx.enter_context(tc.tile_pool(name="halves", bufs=2))
+        quant = ctx.enter_context(tc.tile_pool(name="quant", bufs=2))
+        results = ctx.enter_context(tc.tile_pool(name="results", bufs=3))
+        psum_turn = ctx.enter_context(tc.psum_pool(name="psum_turn", bufs=4))
+        psum_acc = ctx.enter_context(tc.psum_pool(name="psum_acc", bufs=4))
+
+        x_sb = keep.tile([P, TOKENS // P, FEATURES], BF16)
+        for c in range(CHUNKS):
+            nc.sync.dma_start(
+                out=x_sb[:, 2 * c : 2 * c + 2, :],
+                in_=x_rows[c * CHUNK_TOKENS : (c + 1) * CHUNK_TOKENS, :].rearrange(
+                    "(a r) i -> r a i", r=P
+                ),
+            )
+        sp_sb = keep.tile([P, OUTPUTS // P, FEATURES], BF16)
+        nc.sync.dma_start(out=sp_sb, in_=scale_sp.rearrange("(a r) i -> r a i", r=P))
+        coef_sb = keep.tile([P, OUTPUTS // P, FEATURES * NB], BF16)
+        for a in range(OUTPUTS // P):
+            nc.sync.dma_start(
+                out=coef_sb[:, a, :],
+                in_=coef[a * P : (a + 1) * P, :, :].rearrange("r i b -> r (i b)"),
+            )
+        base_words = keep.tile([P, OUTPUTS * PACK], U8, align_bytes=64)
+        nc.sync.dma_start(
+            out=base_words.bitcast(I32),
+            in_=scale_base_words.rearrange("g p n t -> (g p) (n t)").bitcast(I32),
+        )
+        base_planes = keep.tile([P, OUTPUTS], U8, align_bytes=64)
+        nc.vector.memset(base_planes.bitcast(I32), 0)
+        base_scale_rows = scale_base_scales.rearrange("g q n -> (g q) n")
+        for quadrant in range(4):
+            nc.sync.dma_start(
+                out=base_planes[32 * quadrant : 32 * quadrant + 4, :].bitcast(I32),
+                in_=base_scale_rows[4 * quadrant : 4 * quadrant + 4, :].bitcast(I32),
+            )
+        bias_all = keep.tile([P, OUTPUTS], BF16)
+        nc.sync.dma_start(out=bias_all, in_=bias.partition_broadcast(P))
+
+        ident = keep.tile([P, P], F32)
+        make_identity(nc, ident)
+
+        def bias_column(name, value):
+            column = keep.tile([P, 1], F32, name=name)
+            nc.vector.memset(column, value)
+            return column
+
+        plus_half = bias_column("plus_half", 0.5)
+        minus_half = bias_column("minus_half", -0.5)
+        minus_one = bias_column("minus_one", -1.0)
+        minus_two = bias_column("minus_two", -2.0)
+        tail_bias = keep.tile([P, 1], F32)
+        nc.vector.tensor_scalar(
+            out=tail_bias, in0=minus_two, scalar1=TAIL_SCALE, scalar2=None, op0=ALU.mult
+        )
+        minus_two_thirds = keep.tile([P, 1], F32)
+        nc.vector.tensor_scalar(
+            out=minus_two_thirds, in0=minus_two, scalar1=1.0 / 3.0, scalar2=None, op0=ALU.mult
+        )
+
+        x_t = keep.tile([P, TOKENS * PACK], BF16)
+        for c in range(CHUNKS):
+            features_to_partitions(
+                nc,
+                psum_turn,
+                x_sb[:, 2 * c : 2 * c + 2, :],
+                ident,
+                x_t[:, c * CHUNK : (c + 1) * CHUNK],
+            )
+
+        sp_t = keep.tile([P, OUTPUTS * PACK], BF16)
+        for pair in range(OUTPUTS // (2 * P)):
+            features_to_partitions(
+                nc,
+                psum_turn,
+                sp_sb[:, 2 * pair : 2 * pair + 2, :],
+                ident,
+                sp_t[:, pair * 2 * P * PACK : (pair + 1) * 2 * P * PACK],
+            )
+        w_bf = keep.tile([P, NB, OUTPUTS * PACK], BF16, align_bytes=64)
+        for a in range(OUTPUTS // P):
+            o_cols = slice(a * P * PACK, (a + 1) * P * PACK)
+            words = coef_sb[:, a, :].bitcast(F32).rearrange(
+                "r (p t h) -> r p t h", t=PACK, h=NB // 2
+            )
+            for h in range(NB // 2):
+                bank = psum_turn.tile([P, PACK, P], F32, tag="bank")
+                for t in range(PACK):
+                    nc.tensor.transpose(bank[:, t, :], words[:, :, t, h], ident)
+                nc.vector.tensor_tensor(
+                    out=w_bf[:, 2 * h : 2 * h + 2, o_cols].rearrange(
+                        "p e (o t) -> p e o t", t=PACK
+                    ),
+                    in0=bank.bitcast(BF16).rearrange("p t (o e) -> p e o t", e=2),
+                    in1=sp_t[:, o_cols]
+                    .rearrange("p (o t) -> p o t", t=PACK)
+                    .unsqueeze(1)
+                    .to_broadcast([P, 2, P, PACK]),
+                    op=ALU.mult,
+                )
+        w_codes = keep.tile([P, NB, OUTPUTS], U32, align_bytes=64)
+        w_planes = keep.tile([P, NB, OUTPUTS], U8, align_bytes=64)
+        for b in range(NB):
+            nc.vector.quantize_mx(
+                out=w_codes[:, b, :].bitcast(FP8X4), scales=w_planes[:, b, :], in_=w_bf[:, b, :]
+            )
+
+        for c in range(CHUNKS):
+            x_c = x_t[:, c * CHUNK : (c + 1) * CHUNK]
+
+            def distance(name, source, scale, bias_col):
+                d = dist.tile([P, CHUNK], F32, name=name)
+                nc.scalar.activation(out=d, in_=source, func=ACT.Abs, bias=bias_col, scale=scale)
+                return d
+
+            to_4 = distance("to_4", x_c, 1.5, plus_half)
+            to_2_or_6 = distance("to_2_or_6", to_4, 1.0, minus_two)
+            to_odd = distance("to_odd", to_2_or_6, 1.0, minus_one)
+            to_5 = distance("to_5", x_c, 1.5, minus_half)
+            to_3_or_7 = distance("to_3_or_7", to_5, 1.0, minus_two)
+
+            cube = squares.tile([P, CHUNK], F32, tag="square")
+            nc.scalar.activation(out=cube, in_=to_odd, func=ACT.Square)
+            nc.vector.scalar_tensor_tensor(
+                out=cube, in0=to_odd, scalar=2.0, in1=cube, op0=ALU.subtract, op1=ALU.mult
+            )
+            neg_core_odd = halves.tile([P, CHUNK], BF16)
+            nc.scalar.activation(
+                out=neg_core_odd, in_=cube, func=ACT.Identity, bias=minus_two_thirds, scale=-0.5
+            )
+            cube = squares.tile([P, CHUNK], F32, tag="square")
+            nc.scalar.activation(out=cube, in_=to_odd, func=ACT.Square, bias=minus_one)
+            nc.vector.scalar_tensor_tensor(
+                out=cube, in0=to_odd, scalar=1.0, in1=cube, op0=ALU.add, op1=ALU.mult
+            )
+            neg_core_even = halves.tile([P, CHUNK], BF16)
+            nc.scalar.activation(
+                out=neg_core_even, in_=cube, func=ACT.Identity, bias=minus_two_thirds, scale=0.5
+            )
+
+            acts = quant.tile([P, NB + 1, CHUNK], BF16, align_bytes=64)
+            codes = quant.tile([P, NB + 1, CHUNK_TOKENS], U32, align_bytes=64)
+            planes = quant.tile([P, NB + 1, CHUNK_TOKENS], U8, align_bytes=64)
+
+            def quantise(slot):
+                nc.vector.quantize_mx(
+                    out=codes[:, slot, :].bitcast(FP8X4),
+                    scales=planes[:, slot, :],
+                    in_=acts[:, slot, :],
+                )
+
+            def spline(a, neg_core, result):
+                square = squares.tile([P, CHUNK], F32, tag="square")
+                nc.scalar.activation(
+                    out=square, in_=a, func=ACT.Square, bias=tail_bias, scale=TAIL_SCALE
+                )
+                neg = halves.tile([P, CHUNK], BF16, tag="neg", bufs=3)
+                nc.vector.scalar_tensor_tensor(
+                    out=neg, in0=a, scalar=2.0, in1=square, op0=ALU.subtract, op1=ALU.mult
+                )
+                nc.vector.tensor_tensor(out=neg, in0=neg, in1=neg_core, op=ALU.max)
+                nc.vector.tensor_scalar(
+                    out=result, in0=neg, scalar1=-1.0, scalar2=0.0, op0=ALU.mult, op1=ALU.max
+                )
+
+            def spline_pair(a, neg_core, x_between, low, high):
+                both = halves.tile([P, CHUNK], BF16, tag="both")
+                spline(a, neg_core, both)
+                is_low = halves.tile([P, CHUNK], BF16, tag="is_low")
+                nc.vector.tensor_scalar(
+                    out=is_low, in0=x_c, scalar1=x_between, scalar2=None, op0=ALU.is_lt
+                )
+                nc.vector.tensor_tensor(out=low, in0=both, in1=is_low, op=ALU.mult)
+                nc.vector.tensor_tensor(out=high, in0=both, in1=low, op=ALU.subtract)
+
+            nc.scalar.activation(out=acts[:, NB, :], in_=x_c, func=ACT.Silu)
+            spline_pair(to_2_or_6, neg_core_even, -1.0 / 3.0, acts[:, 0, :], acts[:, 4, :])
+            quantise(NB)
+            spline(to_4, neg_core_even, acts[:, 2, :])
+            quantise(0)
+            quantise(4)
+            spline_pair(to_3_or_7, neg_core_odd, 1.0 / 3.0, acts[:, 1, :], acts[:, 5, :])
+            quantise(2)
+            spline(to_5, neg_core_odd, acts[:, 3, :])
+            quantise(1)
+            quantise(5)
+            quantise(3)
+
+            for j in range(CHUNK_TOKENS // P):
+                in_chunk = slice(j * P, (j + 1) * P)
+                first = c * CHUNK_TOKENS + j * P
+                acc = psum_acc.tile([P, OUTPUTS], F32)
+                nc.tensor.matmul_mx(
+                    out=acc,
+                    lhsT=codes[:, NB, in_chunk].bitcast(FP8X4),
+                    lhsT_scale=planes[:, NB, in_chunk],
+                    rhs=base_words.bitcast(FP8X4),
+                    rhs_scale=base_planes,
+                    start=True,
+                    stop=False,
+                )
+                for b in MADE_IN_ORDER:
+                    nc.tensor.matmul_mx(
+                        out=acc,
+                        lhsT=codes[:, b, in_chunk].bitcast(FP8X4),
+                        lhsT_scale=planes[:, b, in_chunk],
+                        rhs=w_codes[:, b, :].bitcast(FP8X4),
+                        rhs_scale=w_planes[:, b, :],
+                        start=False,
+                        stop=(b == MADE_IN_ORDER[-1]),
+                    )
+                result = results.tile([P, OUTPUTS], F32)
+                nc.vector.tensor_tensor(out=result, in0=acc, in1=bias_all, op=ALU.add)
+                nc.sync.dma_start(out=out_rows[first : first + P, :], in_=result)

@@ -21,19 +21,27 @@ NB = 6
 CHUNK_TOKENS = 256
 CHUNK = CHUNK_TOKENS * PACK
 CHUNKS = TOKENS // CHUNK_TOKENS
-MADE_IN_ORDER = (0, 4, 2, 1, 5, 3)
+
 TAIL_SCALE = 6.0 ** -0.5
+RHO = (4.0 ** (1.0 / 3.0) + 16.0 ** (1.0 / 3.0) - 2.0) / 3.0
+ALPHA = 1.0 + RHO / 2.0
+BETA = RHO * (2.0 + RHO) - ALPHA * ALPHA
+CORE_SCALE = 0.5 ** 0.5
+assert all(
+    abs((d + RHO) * ((d - ALPHA) ** 2 + BETA) / 2.0 - (2.0 / 3.0 - d * d + d ** 3 / 2.0)) < 1e-14
+    for d in (0.0, 0.25, 0.5, 1.0, 2.0)
+)
 
 FLOPS = 2 * TOKENS * FEATURES * OUTPUTS * (NB + 1)
 
 
-def features_to_partitions(nc, psum, rows, ident, turned):
+def features_to_partitions(nc, psum, rows, ident, copy, turned):
     bank = psum.tile([P, 2, 2 * P], F32, tag="bank")
     for a in range(2):
         words = rows[:, a, :].bitcast(F32)
         for h in range(2):
             nc.tensor.transpose(bank[:, h, a * P : (a + 1) * P], words[:, h::2], ident)
-    nc.vector.tensor_copy(
+    copy(
         out=turned.bitcast(F32).rearrange("p (r h) -> p r h", h=2),
         in_=bank.rearrange("p h r -> p r h"),
     )
@@ -48,22 +56,24 @@ def tile_kanoriginal_kernel(
 
     with ExitStack() as ctx:
         keep = ctx.enter_context(tc.tile_pool(name="keep", bufs=1))
-        dist = ctx.enter_context(tc.tile_pool(name="dist", bufs=2))
-        squares = ctx.enter_context(tc.tile_pool(name="squares", bufs=4))
-        halves = ctx.enter_context(tc.tile_pool(name="halves", bufs=2))
+        scalar_out = ctx.enter_context(tc.tile_pool(name="scalar_out", bufs=2))
+        vector_own = ctx.enter_context(tc.tile_pool(name="vector_own", bufs=1))
         quant = ctx.enter_context(tc.tile_pool(name="quant", bufs=2))
-        results = ctx.enter_context(tc.tile_pool(name="results", bufs=3))
         psum_turn = ctx.enter_context(tc.psum_pool(name="psum_turn", bufs=4))
-        psum_acc = ctx.enter_context(tc.psum_pool(name="psum_acc", bufs=4))
+        psum_acc = ctx.enter_context(tc.psum_pool(name="psum_acc", bufs=2))
+        ctx.enter_context(tc.manual_schedule())
 
         x_sb = keep.tile([P, TOKENS // P, FEATURES], BF16)
-        for c in range(CHUNKS):
+
+        def load_x(c):
             nc.sync.dma_start(
                 out=x_sb[:, 2 * c : 2 * c + 2, :],
                 in_=x_rows[c * CHUNK_TOKENS : (c + 1) * CHUNK_TOKENS, :].rearrange(
                     "(a r) i -> r a i", r=P
                 ),
             )
+
+        load_x(0)
         sp_sb = keep.tile([P, OUTPUTS // P, FEATURES], BF16)
         nc.sync.dma_start(out=sp_sb, in_=scale_sp.rearrange("(a r) i -> r a i", r=P))
         coef_sb = keep.tile([P, OUTPUTS // P, FEATURES * NB], BF16)
@@ -72,6 +82,8 @@ def tile_kanoriginal_kernel(
                 out=coef_sb[:, a, :],
                 in_=coef[a * P : (a + 1) * P, :, :].rearrange("r i b -> r (i b)"),
             )
+        for c in range(1, CHUNKS):
+            load_x(c)
         base_words = keep.tile([P, OUTPUTS * PACK], U8, align_bytes=64)
         nc.sync.dma_start(
             out=base_words.bitcast(I32),
@@ -90,176 +102,213 @@ def tile_kanoriginal_kernel(
 
         ident = keep.tile([P, P], F32)
         make_identity(nc, ident)
+        one = keep.tile([P, 1], F32)
+        nc.vector.memset(one, 1.0)
 
         def bias_column(name, value):
             column = keep.tile([P, 1], F32, name=name)
-            nc.vector.memset(column, value)
+            nc.vector.tensor_scalar(
+                out=column, in0=one, scalar1=value, scalar2=None, op0=ALU.mult
+            )
             return column
 
         plus_half = bias_column("plus_half", 0.5)
         minus_half = bias_column("minus_half", -0.5)
         minus_one = bias_column("minus_one", -1.0)
         minus_two = bias_column("minus_two", -2.0)
-        tail_bias = keep.tile([P, 1], F32)
-        nc.vector.tensor_scalar(
-            out=tail_bias, in0=minus_two, scalar1=TAIL_SCALE, scalar2=None, op0=ALU.mult
-        )
-        minus_two_thirds = keep.tile([P, 1], F32)
-        nc.vector.tensor_scalar(
-            out=minus_two_thirds, in0=minus_two, scalar1=1.0 / 3.0, scalar2=None, op0=ALU.mult
-        )
+        tail_bias = bias_column("tail_bias", -2.0 * TAIL_SCALE)
+        line_bias_even = bias_column("line_bias_even", -(1.0 + RHO))
+        line_bias_odd = bias_column("line_bias_odd", -RHO)
+        quad_bias_even = bias_column("quad_bias_even", -(1.0 - ALPHA) * CORE_SCALE)
+        quad_bias_odd = bias_column("quad_bias_odd", -ALPHA * CORE_SCALE)
 
         x_t = keep.tile([P, TOKENS * PACK], BF16)
-        for c in range(CHUNKS):
-            features_to_partitions(
-                nc,
-                psum_turn,
-                x_sb[:, 2 * c : 2 * c + 2, :],
-                ident,
-                x_t[:, c * CHUNK : (c + 1) * CHUNK],
-            )
 
-        sp_t = keep.tile([P, OUTPUTS * PACK], BF16)
-        for pair in range(OUTPUTS // (2 * P)):
-            features_to_partitions(
-                nc,
-                psum_turn,
-                sp_sb[:, 2 * pair : 2 * pair + 2, :],
-                ident,
-                sp_t[:, pair * 2 * P * PACK : (pair + 1) * 2 * P * PACK],
-            )
-        w_bf = keep.tile([P, NB, OUTPUTS * PACK], BF16, align_bytes=64)
-        for a in range(OUTPUTS // P):
-            o_cols = slice(a * P * PACK, (a + 1) * P * PACK)
-            words = coef_sb[:, a, :].bitcast(F32).rearrange(
-                "r (p t h) -> r p t h", t=PACK, h=NB // 2
-            )
-            for h in range(NB // 2):
-                bank = psum_turn.tile([P, PACK, P], F32, tag="bank")
-                for t in range(PACK):
-                    nc.tensor.transpose(bank[:, t, :], words[:, :, t, h], ident)
-                nc.vector.tensor_tensor(
-                    out=w_bf[:, 2 * h : 2 * h + 2, o_cols].rearrange(
-                        "p e (o t) -> p e o t", t=PACK
-                    ),
-                    in0=bank.bitcast(BF16).rearrange("p t (o e) -> p e o t", e=2),
-                    in1=sp_t[:, o_cols]
-                    .rearrange("p (o t) -> p o t", t=PACK)
-                    .unsqueeze(1)
-                    .to_broadcast([P, 2, P, PACK]),
-                    op=ALU.mult,
-                )
-        w_codes = keep.tile([P, NB, OUTPUTS], U32, align_bytes=64)
-        w_planes = keep.tile([P, NB, OUTPUTS], U8, align_bytes=64)
-        for b in range(NB):
-            nc.vector.quantize_mx(
-                out=w_codes[:, b, :].bitcast(FP8X4), scales=w_planes[:, b, :], in_=w_bf[:, b, :]
-            )
-
-        for c in range(CHUNKS):
+        def scalar_part(c):
             x_c = x_t[:, c * CHUNK : (c + 1) * CHUNK]
-
-            def distance(name, source, scale, bias_col):
-                d = dist.tile([P, CHUNK], F32, name=name)
-                nc.scalar.activation(out=d, in_=source, func=ACT.Abs, bias=bias_col, scale=scale)
-                return d
-
-            to_4 = distance("to_4", x_c, 1.5, plus_half)
-            to_2_or_6 = distance("to_2_or_6", to_4, 1.0, minus_two)
-            to_odd = distance("to_odd", to_2_or_6, 1.0, minus_one)
-            to_5 = distance("to_5", x_c, 1.5, minus_half)
-            to_3_or_7 = distance("to_3_or_7", to_5, 1.0, minus_two)
-
-            cube = squares.tile([P, CHUNK], F32, tag="square")
-            nc.scalar.activation(out=cube, in_=to_odd, func=ACT.Square)
-            nc.vector.scalar_tensor_tensor(
-                out=cube, in0=to_odd, scalar=2.0, in1=cube, op0=ALU.subtract, op1=ALU.mult
+            features_to_partitions(
+                nc, psum_turn, x_sb[:, 2 * c : 2 * c + 2, :], ident, nc.scalar.copy, x_c
             )
-            neg_core_odd = halves.tile([P, CHUNK], BF16)
+            away = scalar_out.tile([P, 4, CHUNK], F32)
             nc.scalar.activation(
-                out=neg_core_odd, in_=cube, func=ACT.Identity, bias=minus_two_thirds, scale=-0.5
+                out=away[:, 2, :], in_=x_c, func=ACT.Abs, bias=plus_half, scale=1.5
             )
-            cube = squares.tile([P, CHUNK], F32, tag="square")
-            nc.scalar.activation(out=cube, in_=to_odd, func=ACT.Square, bias=minus_one)
-            nc.vector.scalar_tensor_tensor(
-                out=cube, in0=to_odd, scalar=1.0, in1=cube, op0=ALU.add, op1=ALU.mult
-            )
-            neg_core_even = halves.tile([P, CHUNK], BF16)
             nc.scalar.activation(
-                out=neg_core_even, in_=cube, func=ACT.Identity, bias=minus_two_thirds, scale=0.5
+                out=away[:, 3, :], in_=x_c, func=ACT.Abs, bias=minus_half, scale=1.5
             )
+            silu = scalar_out.tile([P, CHUNK], BF16, align_bytes=64)
+            nc.scalar.activation(out=silu, in_=x_c, func=ACT.Silu)
+            nc.scalar.activation(
+                out=away[:, 0:2, :], in_=away[:, 2:4, :], func=ACT.Abs, bias=minus_two
+            )
+            tail_squares = scalar_out.tile([P, 4, CHUNK], F32)
+            nc.scalar.activation(
+                out=tail_squares[:, 2:4, :], in_=away[:, 2:4, :], func=ACT.Square,
+                bias=tail_bias, scale=TAIL_SCALE,
+            )
+            to_odd = scalar_out.tile([P, CHUNK], F32)
+            nc.scalar.activation(out=to_odd, in_=away[:, 0, :], func=ACT.Abs, bias=minus_one)
+            nc.scalar.activation(
+                out=tail_squares[:, 0:2, :], in_=away[:, 0:2, :], func=ACT.Square,
+                bias=tail_bias, scale=TAIL_SCALE,
+            )
+            line = scalar_out.tile([P, 2, CHUNK], F32, bufs=1)
+            quad = scalar_out.tile([P, 2, CHUNK], F32, bufs=1)
+            nc.scalar.activation(
+                out=line[:, 0, :], in_=to_odd, func=ACT.Identity, bias=line_bias_even
+            )
+            nc.scalar.activation(
+                out=line[:, 1, :], in_=to_odd, func=ACT.Identity, bias=line_bias_odd, scale=-1.0
+            )
+            nc.scalar.activation(
+                out=quad[:, 0, :], in_=to_odd, func=ACT.Square,
+                bias=quad_bias_even, scale=CORE_SCALE,
+            )
+            nc.scalar.activation(
+                out=quad[:, 1, :], in_=to_odd, func=ACT.Square,
+                bias=quad_bias_odd, scale=CORE_SCALE,
+            )
+            return silu, away, tail_squares, line, quad
 
-            acts = quant.tile([P, NB + 1, CHUNK], BF16, align_bytes=64)
+        def vector_part(c, silu, away, tail_squares, line, quad):
+            x_c = x_t[:, c * CHUNK : (c + 1) * CHUNK]
+            pairs, singles = slice(0, 2), slice(2, 4)
             codes = quant.tile([P, NB + 1, CHUNK_TOKENS], U32, align_bytes=64)
             planes = quant.tile([P, NB + 1, CHUNK_TOKENS], U8, align_bytes=64)
 
-            def quantise(slot):
+            def quantise(values, slots):
                 nc.vector.quantize_mx(
-                    out=codes[:, slot, :].bitcast(FP8X4),
-                    scales=planes[:, slot, :],
-                    in_=acts[:, slot, :],
+                    out=codes[:, slots, :].rearrange("p s n -> p (s n)").bitcast(FP8X4),
+                    scales=planes[:, slots, :].rearrange("p s n -> p (s n)"),
+                    in_=values,
                 )
 
-            def spline(a, neg_core, result):
-                square = squares.tile([P, CHUNK], F32, tag="square")
-                nc.scalar.activation(
-                    out=square, in_=a, func=ACT.Square, bias=tail_bias, scale=TAIL_SCALE
-                )
-                neg = halves.tile([P, CHUNK], BF16, tag="neg", bufs=3)
+            neg = vector_own.tile([P, 4, CHUNK], BF16)
+            for kind in (singles, pairs):
                 nc.vector.scalar_tensor_tensor(
-                    out=neg, in0=a, scalar=2.0, in1=square, op0=ALU.subtract, op1=ALU.mult
+                    out=neg[:, kind, :], in0=away[:, kind, :], scalar=2.0,
+                    in1=tail_squares[:, kind, :], op0=ALU.subtract, op1=ALU.mult,
                 )
-                nc.vector.tensor_tensor(out=neg, in0=neg, in1=neg_core, op=ALU.max)
+            neg_core = vector_own.tile([P, 2, CHUNK], BF16)
+            nc.vector.scalar_tensor_tensor(
+                out=neg_core, in0=quad, scalar=BETA / 2.0, in1=line, op0=ALU.add, op1=ALU.mult
+            )
+            is_low = vector_own.tile([P, 2, CHUNK], BF16)
+            nc.vector.tensor_scalar(
+                out=is_low[:, 0, :], in0=x_c, scalar1=-1.0 / 3.0, scalar2=None, op0=ALU.is_lt
+            )
+            nc.vector.tensor_scalar(
+                out=is_low[:, 1, :], in0=x_c, scalar1=1.0 / 3.0, scalar2=None, op0=ALU.is_lt
+            )
+            for kind in (singles, pairs):
+                nc.vector.tensor_tensor(
+                    out=neg[:, kind, :], in0=neg[:, kind, :], in1=neg_core, op=ALU.max
+                )
+            basis = vector_own.tile([P, NB, CHUNK], BF16, align_bytes=64)
+            both = neg[:, pairs, :]
+            for result, kind in ((basis[:, 2:4, :], singles), (both, pairs)):
                 nc.vector.tensor_scalar(
-                    out=result, in0=neg, scalar1=-1.0, scalar2=0.0, op0=ALU.mult, op1=ALU.max
+                    out=result, in0=neg[:, kind, :], scalar1=-1.0, scalar2=0.0,
+                    op0=ALU.mult, op1=ALU.max,
                 )
+            quantise(basis[:, 2:4, :].rearrange("p s m -> p (s m)"), slice(2, 4))
+            nc.vector.tensor_tensor(out=basis[:, 0:2, :], in0=both, in1=is_low, op=ALU.mult)
+            quantise(silu, slice(NB, NB + 1))
+            nc.vector.tensor_tensor(
+                out=basis[:, 4:6, :], in0=both, in1=basis[:, 0:2, :], op=ALU.subtract
+            )
+            quantise(basis[:, 0:2, :].rearrange("p s m -> p (s m)"), slice(0, 2))
+            quantise(basis[:, 4:6, :].rearrange("p s m -> p (s m)"), slice(4, 6))
+            return codes, planes
 
-            def spline_pair(a, neg_core, x_between, low, high):
-                both = halves.tile([P, CHUNK], BF16, tag="both")
-                spline(a, neg_core, both)
-                is_low = halves.tile([P, CHUNK], BF16, tag="is_low")
-                nc.vector.tensor_scalar(
-                    out=is_low, in0=x_c, scalar1=x_between, scalar2=None, op0=ALU.is_lt
+        w_codes = keep.tile([P, NB, OUTPUTS], U32, align_bytes=64)
+        w_planes = keep.tile([P, NB, OUTPUTS], U8, align_bytes=64)
+
+        def make_weights():
+            def quantise_piece(piece, a, h):
+                for e in range(2):
+                    nc.vector.quantize_mx(
+                        out=w_codes[:, 2 * h + e, a * P : (a + 1) * P].bitcast(FP8X4),
+                        scales=w_planes[:, 2 * h + e, a * P : (a + 1) * P],
+                        in_=piece[:, e, :],
+                    )
+
+            sp_t = keep.tile([P, OUTPUTS * PACK], BF16)
+            for pair in range(OUTPUTS // (2 * P)):
+                features_to_partitions(
+                    nc,
+                    psum_turn,
+                    sp_sb[:, 2 * pair : 2 * pair + 2, :],
+                    ident,
+                    nc.vector.tensor_copy,
+                    sp_t[:, pair * 2 * P * PACK : (pair + 1) * 2 * P * PACK],
                 )
-                nc.vector.tensor_tensor(out=low, in0=both, in1=is_low, op=ALU.mult)
-                nc.vector.tensor_tensor(out=high, in0=both, in1=low, op=ALU.subtract)
+            waiting = None
+            for a in range(OUTPUTS // P):
+                words = coef_sb[:, a, :].bitcast(F32).rearrange(
+                    "r (p t h) -> r p t h", t=PACK, h=NB // 2
+                )
+                for h in range(NB // 2):
+                    bank = psum_turn.tile([P, PACK, P], F32, tag="bank")
+                    for t in range(PACK):
+                        nc.tensor.transpose(bank[:, t, :], words[:, :, t, h], ident)
+                    piece = vector_own.tile([P, 2, P * PACK], BF16, bufs=2, align_bytes=64)
+                    nc.vector.tensor_tensor(
+                        out=piece.rearrange("p e (o t) -> p e o t", t=PACK),
+                        in0=bank.bitcast(BF16).rearrange("p t (o e) -> p e o t", e=2),
+                        in1=sp_t[:, a * P * PACK : (a + 1) * P * PACK]
+                        .rearrange("p (o t) -> p o t", t=PACK)
+                        .unsqueeze(1)
+                        .to_broadcast([P, 2, P, PACK]),
+                        op=ALU.mult,
+                    )
+                    if waiting is not None:
+                        quantise_piece(*waiting)
+                    waiting = (piece, a, h)
+            quantise_piece(*waiting)
 
-            nc.scalar.activation(out=acts[:, NB, :], in_=x_c, func=ACT.Silu)
-            spline_pair(to_2_or_6, neg_core_even, -1.0 / 3.0, acts[:, 0, :], acts[:, 4, :])
-            quantise(NB)
-            spline(to_4, neg_core_even, acts[:, 2, :])
-            quantise(0)
-            quantise(4)
-            spline_pair(to_3_or_7, neg_core_odd, 1.0 / 3.0, acts[:, 1, :], acts[:, 5, :])
-            quantise(2)
-            spline(to_5, neg_core_odd, acts[:, 3, :])
-            quantise(1)
-            quantise(5)
-            quantise(3)
+        token_tiles = range(CHUNK_TOKENS // P)
 
-            for j in range(CHUNK_TOKENS // P):
-                in_chunk = slice(j * P, (j + 1) * P)
-                first = c * CHUNK_TOKENS + j * P
-                acc = psum_acc.tile([P, OUTPUTS], F32)
+        def multiply(codes, planes):
+            sums = [psum_acc.tile([P, OUTPUTS], F32, name="sum%d" % j) for j in token_tiles]
+            for j in token_tiles:
                 nc.tensor.matmul_mx(
-                    out=acc,
-                    lhsT=codes[:, NB, in_chunk].bitcast(FP8X4),
-                    lhsT_scale=planes[:, NB, in_chunk],
+                    out=sums[j],
+                    lhsT=codes[:, NB, j * P : (j + 1) * P].bitcast(FP8X4),
+                    lhsT_scale=planes[:, NB, j * P : (j + 1) * P],
                     rhs=base_words.bitcast(FP8X4),
                     rhs_scale=base_planes,
                     start=True,
                     stop=False,
                 )
-                for b in MADE_IN_ORDER:
+            for b in range(NB):
+                for j in token_tiles:
                     nc.tensor.matmul_mx(
-                        out=acc,
-                        lhsT=codes[:, b, in_chunk].bitcast(FP8X4),
-                        lhsT_scale=planes[:, b, in_chunk],
+                        out=sums[j],
+                        lhsT=codes[:, b, j * P : (j + 1) * P].bitcast(FP8X4),
+                        lhsT_scale=planes[:, b, j * P : (j + 1) * P],
                         rhs=w_codes[:, b, :].bitcast(FP8X4),
                         rhs_scale=w_planes[:, b, :],
                         start=False,
-                        stop=(b == MADE_IN_ORDER[-1]),
+                        stop=(b == NB - 1),
                     )
-                result = results.tile([P, OUTPUTS], F32)
-                nc.vector.tensor_tensor(out=result, in0=acc, in1=bias_all, op=ALU.add)
+            return sums
+
+        def finish(c, sums):
+            for j in token_tiles:
+                first = c * CHUNK_TOKENS + j * P
+                result = vector_own.tile([P, OUTPUTS], F32, bufs=2)
+                nc.vector.tensor_tensor(out=result, in0=sums[j], in1=bias_all, op=ALU.add)
                 nc.sync.dma_start(out=out_rows[first : first + P, :], in_=result)
+
+        made = scalar_part(0)
+        make_weights()
+        sums = None
+        for c in range(CHUNKS):
+            ahead = scalar_part(c + 1) if c + 1 < CHUNKS else None
+            codes, planes = vector_part(c, *made)
+            if c > 0:
+                finish(c - 1, sums)
+            sums = multiply(codes, planes)
+            made = ahead
+        finish(CHUNKS - 1, sums)

@@ -18,9 +18,12 @@ TOKENS = 1024
 FEATURES = 512
 OUTPUTS = 512
 NB = 6
-CHUNK_TOKENS = 256
-CHUNK = CHUNK_TOKENS * PACK
-CHUNKS = TOKENS // CHUNK_TOKENS
+SLOTS = NB + 1
+CHUNK_TILES = 2
+CHUNK_ROWS = CHUNK_TILES * P
+CHUNK = CHUNK_ROWS * PACK
+CHUNKS = TOKENS // CHUNK_ROWS
+QUANTISED_IN_ORDER = (2, 3, NB, 0, 1, 4, 5)
 
 TAIL_SCALE = 6.0 ** -0.5
 RHO = (4.0 ** (1.0 / 3.0) + 16.0 ** (1.0 / 3.0) - 2.0) / 3.0
@@ -32,12 +35,12 @@ assert all(
     for d in (0.0, 0.25, 0.5, 1.0, 2.0)
 )
 
-FLOPS = 2 * TOKENS * FEATURES * OUTPUTS * (NB + 1)
+FLOPS = 2 * TOKENS * FEATURES * OUTPUTS * SLOTS
 
 
 def features_to_partitions(nc, psum, rows, ident, copy, turned):
-    bank = psum.tile([P, 2, 2 * P], F32, tag="bank")
-    for a in range(2):
+    bank = psum.tile([P, 2, CHUNK_ROWS], F32, tag="bank")
+    for a in range(CHUNK_TILES):
         words = rows[:, a, :].bitcast(F32)
         for h in range(2):
             nc.tensor.transpose(bank[:, h, a * P : (a + 1) * P], words[:, h::2], ident)
@@ -58,17 +61,16 @@ def tile_kanoriginal_kernel(
         keep = ctx.enter_context(tc.tile_pool(name="keep", bufs=1))
         scalar_out = ctx.enter_context(tc.tile_pool(name="scalar_out", bufs=2))
         vector_own = ctx.enter_context(tc.tile_pool(name="vector_own", bufs=1))
-        quant = ctx.enter_context(tc.tile_pool(name="quant", bufs=2))
+        vector_out = ctx.enter_context(tc.tile_pool(name="vector_out", bufs=2))
         psum_turn = ctx.enter_context(tc.psum_pool(name="psum_turn", bufs=4))
-        psum_acc = ctx.enter_context(tc.psum_pool(name="psum_acc", bufs=2))
-        ctx.enter_context(tc.manual_schedule())
+        psum_sums = ctx.enter_context(tc.psum_pool(name="psum_sums", bufs=2))
 
         x_sb = keep.tile([P, TOKENS // P, FEATURES], BF16)
 
         def load_x(c):
             nc.sync.dma_start(
-                out=x_sb[:, 2 * c : 2 * c + 2, :],
-                in_=x_rows[c * CHUNK_TOKENS : (c + 1) * CHUNK_TOKENS, :].rearrange(
+                out=x_sb[:, c * CHUNK_TILES : (c + 1) * CHUNK_TILES, :],
+                in_=x_rows[c * CHUNK_ROWS : (c + 1) * CHUNK_ROWS, :].rearrange(
                     "(a r) i -> r a i", r=P
                 ),
             )
@@ -84,17 +86,17 @@ def tile_kanoriginal_kernel(
             )
         for c in range(1, CHUNKS):
             load_x(c)
-        base_words = keep.tile([P, OUTPUTS * PACK], U8, align_bytes=64)
+        w_codes = keep.tile([P, SLOTS, OUTPUTS], U32, align_bytes=64)
+        w_planes = keep.tile([P, SLOTS, OUTPUTS], U8, align_bytes=64)
         nc.sync.dma_start(
-            out=base_words.bitcast(I32),
+            out=w_codes[:, NB, :].bitcast(I32),
             in_=scale_base_words.rearrange("g p n t -> (g p) (n t)").bitcast(I32),
         )
-        base_planes = keep.tile([P, OUTPUTS], U8, align_bytes=64)
-        nc.vector.memset(base_planes.bitcast(I32), 0)
+        nc.vector.memset(w_planes[:, NB, :].bitcast(I32), 0)
         base_scale_rows = scale_base_scales.rearrange("g q n -> (g q) n")
         for quadrant in range(4):
             nc.sync.dma_start(
-                out=base_planes[32 * quadrant : 32 * quadrant + 4, :].bitcast(I32),
+                out=w_planes[32 * quadrant : 32 * quadrant + 4, NB, :].bitcast(I32),
                 in_=base_scale_rows[4 * quadrant : 4 * quadrant + 4, :].bitcast(I32),
             )
         bias_all = keep.tile([P, OUTPUTS], BF16)
@@ -127,7 +129,12 @@ def tile_kanoriginal_kernel(
         def scalar_part(c):
             x_c = x_t[:, c * CHUNK : (c + 1) * CHUNK]
             features_to_partitions(
-                nc, psum_turn, x_sb[:, 2 * c : 2 * c + 2, :], ident, nc.scalar.copy, x_c
+                nc,
+                psum_turn,
+                x_sb[:, c * CHUNK_TILES : (c + 1) * CHUNK_TILES, :],
+                ident,
+                nc.scalar.copy,
+                x_c,
             )
             away = scalar_out.tile([P, 4, CHUNK], F32)
             nc.scalar.activation(
@@ -173,8 +180,8 @@ def tile_kanoriginal_kernel(
         def vector_part(c, silu, away, tail_squares, line, quad):
             x_c = x_t[:, c * CHUNK : (c + 1) * CHUNK]
             pairs, singles = slice(0, 2), slice(2, 4)
-            codes = quant.tile([P, NB + 1, CHUNK_TOKENS], U32, align_bytes=64)
-            planes = quant.tile([P, NB + 1, CHUNK_TOKENS], U8, align_bytes=64)
+            codes = vector_out.tile([P, SLOTS, CHUNK_ROWS], U32, align_bytes=64)
+            planes = vector_out.tile([P, SLOTS, CHUNK_ROWS], U8, align_bytes=64)
 
             def quantise(values, slots):
                 nc.vector.quantize_mx(
@@ -206,23 +213,20 @@ def tile_kanoriginal_kernel(
                 )
             basis = vector_own.tile([P, NB, CHUNK], BF16, align_bytes=64)
             both = neg[:, pairs, :]
-            for result, kind in ((basis[:, 2:4, :], singles), (both, pairs)):
+            for cut, kind in ((basis[:, 2:4, :], singles), (both, pairs)):
                 nc.vector.tensor_scalar(
-                    out=result, in0=neg[:, kind, :], scalar1=-1.0, scalar2=0.0,
+                    out=cut, in0=neg[:, kind, :], scalar1=-1.0, scalar2=0.0,
                     op0=ALU.mult, op1=ALU.max,
                 )
             quantise(basis[:, 2:4, :].rearrange("p s m -> p (s m)"), slice(2, 4))
             nc.vector.tensor_tensor(out=basis[:, 0:2, :], in0=both, in1=is_low, op=ALU.mult)
-            quantise(silu, slice(NB, NB + 1))
+            quantise(silu, slice(NB, SLOTS))
             nc.vector.tensor_tensor(
                 out=basis[:, 4:6, :], in0=both, in1=basis[:, 0:2, :], op=ALU.subtract
             )
             quantise(basis[:, 0:2, :].rearrange("p s m -> p (s m)"), slice(0, 2))
             quantise(basis[:, 4:6, :].rearrange("p s m -> p (s m)"), slice(4, 6))
             return codes, planes
-
-        w_codes = keep.tile([P, NB, OUTPUTS], U32, align_bytes=64)
-        w_planes = keep.tile([P, NB, OUTPUTS], U8, align_bytes=64)
 
         def make_weights():
             def quantise_piece(piece, a, h):
@@ -234,14 +238,14 @@ def tile_kanoriginal_kernel(
                     )
 
             sp_t = keep.tile([P, OUTPUTS * PACK], BF16)
-            for pair in range(OUTPUTS // (2 * P)):
+            for c in range(OUTPUTS // CHUNK_ROWS):
                 features_to_partitions(
                     nc,
                     psum_turn,
-                    sp_sb[:, 2 * pair : 2 * pair + 2, :],
+                    sp_sb[:, c * CHUNK_TILES : (c + 1) * CHUNK_TILES, :],
                     ident,
                     nc.vector.tensor_copy,
-                    sp_t[:, pair * 2 * P * PACK : (pair + 1) * 2 * P * PACK],
+                    sp_t[:, c * CHUNK : (c + 1) * CHUNK],
                 )
             waiting = None
             for a in range(OUTPUTS // P):
@@ -267,37 +271,27 @@ def tile_kanoriginal_kernel(
                     waiting = (piece, a, h)
             quantise_piece(*waiting)
 
-        token_tiles = range(CHUNK_TOKENS // P)
+        token_tiles = range(CHUNK_TILES)
 
         def multiply(codes, planes):
-            sums = [psum_acc.tile([P, OUTPUTS], F32, name="sum%d" % j) for j in token_tiles]
-            for j in token_tiles:
-                nc.tensor.matmul_mx(
-                    out=sums[j],
-                    lhsT=codes[:, NB, j * P : (j + 1) * P].bitcast(FP8X4),
-                    lhsT_scale=planes[:, NB, j * P : (j + 1) * P],
-                    rhs=base_words.bitcast(FP8X4),
-                    rhs_scale=base_planes,
-                    start=True,
-                    stop=False,
-                )
-            for b in range(NB):
+            sums = [psum_sums.tile([P, OUTPUTS], F32, name="sum%d" % j) for j in token_tiles]
+            for slot in QUANTISED_IN_ORDER:
                 for j in token_tiles:
                     nc.tensor.matmul_mx(
                         out=sums[j],
-                        lhsT=codes[:, b, j * P : (j + 1) * P].bitcast(FP8X4),
-                        lhsT_scale=planes[:, b, j * P : (j + 1) * P],
-                        rhs=w_codes[:, b, :].bitcast(FP8X4),
-                        rhs_scale=w_planes[:, b, :],
-                        start=False,
-                        stop=(b == NB - 1),
+                        lhsT=codes[:, slot, j * P : (j + 1) * P].bitcast(FP8X4),
+                        lhsT_scale=planes[:, slot, j * P : (j + 1) * P],
+                        rhs=w_codes[:, slot, :].bitcast(FP8X4),
+                        rhs_scale=w_planes[:, slot, :],
+                        start=(slot == QUANTISED_IN_ORDER[0]),
+                        stop=(slot == QUANTISED_IN_ORDER[-1]),
                     )
             return sums
 
         def finish(c, sums):
             for j in token_tiles:
-                first = c * CHUNK_TOKENS + j * P
-                result = vector_own.tile([P, OUTPUTS], F32, bufs=2)
+                first = c * CHUNK_ROWS + j * P
+                result = vector_out.tile([P, OUTPUTS], F32)
                 nc.vector.tensor_tensor(out=result, in0=sums[j], in1=bias_all, op=ALU.add)
                 nc.sync.dma_start(out=out_rows[first : first + P, :], in_=result)
 

@@ -21,6 +21,9 @@ NB = 6
 SLOTS = NB + 1
 CHUNK_TILES = 2
 CHUNK_ROWS = CHUNK_TILES * P
+HALF = FEATURES // 2
+HALF_ROWS = P // 2
+CHUNK_HALF_TILES = CHUNK_ROWS // HALF_ROWS
 CHUNK = CHUNK_ROWS * PACK
 CHUNKS = TOKENS // CHUNK_ROWS
 QUANTISED_IN_ORDER = (2, 3, NB, 0, 1, 4, 5)
@@ -38,16 +41,13 @@ assert all(
 FLOPS = 2 * TOKENS * FEATURES * OUTPUTS * SLOTS
 
 
-def features_to_partitions(nc, psum, rows, ident, copy, turned):
-    bank = psum.tile([P, 2, CHUNK_ROWS], F32, tag="bank")
-    for a in range(CHUNK_TILES):
-        words = rows[:, a, :].bitcast(F32)
-        for h in range(2):
-            nc.tensor.transpose(bank[:, h, a * P : (a + 1) * P], words[:, h::2], ident)
-    copy(
-        out=turned.bitcast(F32).rearrange("p (r h) -> p r h", h=2),
-        in_=bank.rearrange("p h r -> p r h"),
-    )
+def turn_half_rows(nc, out, half_rows, ident):
+    for e in range(2):
+        nc.tensor.transpose(
+            out.rearrange("p (r e u) -> p e r u", e=2, u=2)[:, e],
+            half_rows.rearrange("k (p e) -> k e p", e=2)[:, e, :],
+            ident,
+        )
 
 
 def tile_kanoriginal_kernel(
@@ -62,10 +62,21 @@ def tile_kanoriginal_kernel(
         scalar_out = ctx.enter_context(tc.tile_pool(name="scalar_out", bufs=2))
         vector_own = ctx.enter_context(tc.tile_pool(name="vector_own", bufs=1))
         vector_out = ctx.enter_context(tc.tile_pool(name="vector_out", bufs=2))
-        psum_turn = ctx.enter_context(tc.psum_pool(name="psum_turn", bufs=4))
-        psum_sums = ctx.enter_context(tc.psum_pool(name="psum_sums", bufs=2))
+        psum_turn = ctx.enter_context(tc.psum_pool(name="psum_turn", bufs=6))
+        psum_sums = ctx.enter_context(tc.psum_pool(name="psum_sums", bufs=1))
+
+        ctx.enter_context(tc.manual_schedule())
 
         x_sb = keep.tile([P, TOKENS // P, FEATURES], BF16)
+        x_half_sb = keep.tile([P, TOKENS // HALF_ROWS, HALF], BF16)
+        sp_sb = keep.tile([P, OUTPUTS // HALF_ROWS, HALF], BF16)
+        coef_sb = keep.tile([P, OUTPUTS // HALF_ROWS, HALF * NB], BF16)
+        coef_rows = coef.rearrange("o i b -> o (i b)")
+
+        def load_half_rows(out, rows):
+            nc.sync.dma_start(
+                out=out, in_=rows.rearrange("(a r) (u i) -> (r u) a i", r=HALF_ROWS, u=2)
+            )
 
         def load_x(c):
             nc.sync.dma_start(
@@ -75,16 +86,30 @@ def tile_kanoriginal_kernel(
                 ),
             )
 
-        load_x(0)
-        sp_sb = keep.tile([P, OUTPUTS // P, FEATURES], BF16)
-        nc.sync.dma_start(out=sp_sb, in_=scale_sp.rearrange("(a r) i -> r a i", r=P))
-        coef_sb = keep.tile([P, OUTPUTS // P, FEATURES * NB], BF16)
-        for a in range(OUTPUTS // P):
-            nc.sync.dma_start(
-                out=coef_sb[:, a, :],
-                in_=coef[a * P : (a + 1) * P, :, :].rearrange("r i b -> r (i b)"),
+        def load_x_halves(c):
+            load_half_rows(
+                x_half_sb[:, c * CHUNK_HALF_TILES : (c + 1) * CHUNK_HALF_TILES, :],
+                x_rows[c * CHUNK_ROWS : (c + 1) * CHUNK_ROWS, :],
             )
+
+        def load_sp(c):
+            load_half_rows(
+                sp_sb[:, c * CHUNK_HALF_TILES : (c + 1) * CHUNK_HALF_TILES, :],
+                scale_sp[c * CHUNK_ROWS : (c + 1) * CHUNK_ROWS, :],
+            )
+
+        def load_coef(a):
+            load_half_rows(coef_sb[:, 2 * a : 2 * a + 2, :], coef_rows[a * P : (a + 1) * P, :])
+
+        load_x_halves(0)
+        load_sp(0)
+        load_coef(0)
+        load_x(0)
+        load_sp(1)
+        for a in range(1, OUTPUTS // P):
+            load_coef(a)
         for c in range(1, CHUNKS):
+            load_x_halves(c)
             load_x(c)
         w_codes = keep.tile([P, SLOTS, OUTPUTS], U32, align_bytes=64)
         w_planes = keep.tile([P, SLOTS, OUTPUTS], U8, align_bytes=64)
@@ -102,6 +127,8 @@ def tile_kanoriginal_kernel(
         bias_all = keep.tile([P, OUTPUTS], BF16)
         nc.sync.dma_start(out=bias_all, in_=bias.partition_broadcast(P))
 
+        ident_bf = keep.tile([P, P], BF16)
+        make_identity(nc, ident_bf)
         ident = keep.tile([P, P], F32)
         make_identity(nc, ident)
         one = keep.tile([P, 1], F32)
@@ -126,16 +153,28 @@ def tile_kanoriginal_kernel(
 
         x_t = keep.tile([P, TOKENS * PACK], BF16)
 
-        def scalar_part(c):
+        def turn_x(c):
+            bank = psum_turn.tile([P, CHUNK], BF16, tag="bank")
+            for a in range(CHUNK_HALF_TILES):
+                turn_half_rows(
+                    nc,
+                    bank[:, a * HALF : (a + 1) * HALF],
+                    x_half_sb[:, c * CHUNK_HALF_TILES + a, :],
+                    ident_bf,
+                )
+            return bank
+
+        def turn_x_words(c):
+            bank = psum_turn.tile([P, 2, CHUNK_ROWS], F32, tag="bank")
+            for a in range(CHUNK_TILES):
+                words = x_sb[:, c * CHUNK_TILES + a, :].bitcast(F32)
+                for h in range(2):
+                    nc.tensor.transpose(bank[:, h, a * P : (a + 1) * P], words[:, h::2], ident)
+            return bank
+
+        def distances(c, bank):
             x_c = x_t[:, c * CHUNK : (c + 1) * CHUNK]
-            features_to_partitions(
-                nc,
-                psum_turn,
-                x_sb[:, c * CHUNK_TILES : (c + 1) * CHUNK_TILES, :],
-                ident,
-                nc.scalar.copy,
-                x_c,
-            )
+            nc.scalar.copy(out=x_c, in_=bank)
             away = scalar_out.tile([P, 4, CHUNK], F32)
             nc.scalar.activation(
                 out=away[:, 2, :], in_=x_c, func=ACT.Abs, bias=plus_half, scale=1.5
@@ -143,15 +182,22 @@ def tile_kanoriginal_kernel(
             nc.scalar.activation(
                 out=away[:, 3, :], in_=x_c, func=ACT.Abs, bias=minus_half, scale=1.5
             )
-            silu = scalar_out.tile([P, CHUNK], BF16, align_bytes=64)
-            nc.scalar.activation(out=silu, in_=x_c, func=ACT.Silu)
             nc.scalar.activation(
                 out=away[:, 0:2, :], in_=away[:, 2:4, :], func=ACT.Abs, bias=minus_two
             )
+            return away
+
+        def factors(away, words_bank):
             tail_squares = scalar_out.tile([P, 4, CHUNK], F32)
             nc.scalar.activation(
                 out=tail_squares[:, 2:4, :], in_=away[:, 2:4, :], func=ACT.Square,
                 bias=tail_bias, scale=TAIL_SCALE,
+            )
+            silu = scalar_out.tile([P, CHUNK], BF16, align_bytes=64)
+            nc.scalar.activation(
+                out=silu.rearrange("p (r h e) -> p r h e", h=2, e=2),
+                in_=words_bank.bitcast(BF16).rearrange("p h (r e) -> p r h e", e=2),
+                func=ACT.Silu,
             )
             to_odd = scalar_out.tile([P, CHUNK], F32)
             nc.scalar.activation(out=to_odd, in_=away[:, 0, :], func=ACT.Abs, bias=minus_one)
@@ -177,8 +223,18 @@ def tile_kanoriginal_kernel(
             )
             return silu, away, tail_squares, line, quad
 
-        def vector_part(c, silu, away, tail_squares, line, quad):
+        def masks(c):
             x_c = x_t[:, c * CHUNK : (c + 1) * CHUNK]
+            is_low = vector_own.tile([P, 2, CHUNK], BF16)
+            nc.vector.tensor_scalar(
+                out=is_low[:, 0, :], in0=x_c, scalar1=-1.0 / 3.0, scalar2=None, op0=ALU.is_lt
+            )
+            nc.vector.tensor_scalar(
+                out=is_low[:, 1, :], in0=x_c, scalar1=1.0 / 3.0, scalar2=None, op0=ALU.is_lt
+            )
+            return is_low
+
+        def vector_part(is_low, before, silu, away, tail_squares, line, quad):
             pairs, singles = slice(0, 2), slice(2, 4)
             codes = vector_out.tile([P, SLOTS, CHUNK_ROWS], U32, align_bytes=64)
             planes = vector_out.tile([P, SLOTS, CHUNK_ROWS], U8, align_bytes=64)
@@ -196,16 +252,11 @@ def tile_kanoriginal_kernel(
                     out=neg[:, kind, :], in0=away[:, kind, :], scalar=2.0,
                     in1=tail_squares[:, kind, :], op0=ALU.subtract, op1=ALU.mult,
                 )
+            if before is not None:
+                finish(*before)
             neg_core = vector_own.tile([P, 2, CHUNK], BF16)
             nc.vector.scalar_tensor_tensor(
                 out=neg_core, in0=quad, scalar=BETA / 2.0, in1=line, op0=ALU.add, op1=ALU.mult
-            )
-            is_low = vector_own.tile([P, 2, CHUNK], BF16)
-            nc.vector.tensor_scalar(
-                out=is_low[:, 0, :], in0=x_c, scalar1=-1.0 / 3.0, scalar2=None, op0=ALU.is_lt
-            )
-            nc.vector.tensor_scalar(
-                out=is_low[:, 1, :], in0=x_c, scalar1=1.0 / 3.0, scalar2=None, op0=ALU.is_lt
             )
             for kind in (singles, pairs):
                 nc.vector.tensor_tensor(
@@ -228,81 +279,102 @@ def tile_kanoriginal_kernel(
             quantise(basis[:, 4:6, :].rearrange("p s m -> p (s m)"), slice(4, 6))
             return codes, planes
 
-        def make_weights():
-            def quantise_piece(piece, a, h):
-                for e in range(2):
-                    nc.vector.quantize_mx(
-                        out=w_codes[:, 2 * h + e, a * P : (a + 1) * P].bitcast(FP8X4),
-                        scales=w_planes[:, 2 * h + e, a * P : (a + 1) * P],
-                        in_=piece[:, e, :],
-                    )
+        def quantise_piece(piece, a, h):
+            for e in range(2):
+                nc.vector.quantize_mx(
+                    out=w_codes[:, 2 * h + e, a * P : (a + 1) * P].bitcast(FP8X4),
+                    scales=w_planes[:, 2 * h + e, a * P : (a + 1) * P],
+                    in_=piece[:, e, :],
+                )
 
-            sp_t = keep.tile([P, OUTPUTS * PACK], BF16)
-            for c in range(OUTPUTS // CHUNK_ROWS):
-                features_to_partitions(
+        sp_t = keep.tile([P, OUTPUTS * PACK], BF16)
+
+        def turn_sp(c):
+            bank = psum_turn.tile([P, CHUNK], BF16, tag="bank")
+            for a in range(CHUNK_HALF_TILES):
+                turn_half_rows(
                     nc,
-                    psum_turn,
-                    sp_sb[:, c * CHUNK_TILES : (c + 1) * CHUNK_TILES, :],
-                    ident,
-                    nc.vector.tensor_copy,
-                    sp_t[:, c * CHUNK : (c + 1) * CHUNK],
+                    bank[:, a * HALF : (a + 1) * HALF],
+                    sp_sb[:, c * CHUNK_HALF_TILES + a, :],
+                    ident_bf,
                 )
-            waiting = None
-            for a in range(OUTPUTS // P):
-                words = coef_sb[:, a, :].bitcast(F32).rearrange(
-                    "r (p t h) -> r p t h", t=PACK, h=NB // 2
-                )
-                for h in range(NB // 2):
-                    bank = psum_turn.tile([P, PACK, P], F32, tag="bank")
-                    for t in range(PACK):
-                        nc.tensor.transpose(bank[:, t, :], words[:, :, t, h], ident)
-                    piece = vector_own.tile([P, 2, P * PACK], BF16, bufs=2, align_bytes=64)
-                    nc.vector.tensor_tensor(
-                        out=piece.rearrange("p e (o t) -> p e o t", t=PACK),
-                        in0=bank.bitcast(BF16).rearrange("p t (o e) -> p e o t", e=2),
-                        in1=sp_t[:, a * P * PACK : (a + 1) * P * PACK]
-                        .rearrange("p (o t) -> p o t", t=PACK)
-                        .unsqueeze(1)
-                        .to_broadcast([P, 2, P, PACK]),
-                        op=ALU.mult,
+            nc.vector.tensor_copy(out=sp_t[:, c * CHUNK : (c + 1) * CHUNK], in_=bank)
+
+        def weight_piece(a, h):
+            bank = psum_turn.tile([P, 2, P * PACK], BF16, tag="bank")
+            for b in range(2):
+                for half in range(2):
+                    turn_half_rows(
+                        nc,
+                        bank[:, b, half * HALF : (half + 1) * HALF],
+                        coef_sb[:, 2 * a + half, :].rearrange("k (i b) -> k b i", b=NB)[
+                            :, 2 * h + b, :
+                        ],
+                        ident_bf,
                     )
-                    if waiting is not None:
-                        quantise_piece(*waiting)
-                    waiting = (piece, a, h)
-            quantise_piece(*waiting)
+            piece = vector_own.tile([P, 2, P * PACK], BF16, bufs=3, align_bytes=64)
+            nc.vector.tensor_tensor(
+                out=piece,
+                in0=bank,
+                in1=sp_t[:, a * P * PACK : (a + 1) * P * PACK]
+                .unsqueeze(1)
+                .to_broadcast([P, 2, P * PACK]),
+                op=ALU.mult,
+            )
+            return piece, a, h
 
         token_tiles = range(CHUNK_TILES)
 
         def multiply(codes, planes):
             sums = [psum_sums.tile([P, OUTPUTS], F32, name="sum%d" % j) for j in token_tiles]
-            for slot in QUANTISED_IN_ORDER:
-                for j in token_tiles:
-                    nc.tensor.matmul_mx(
-                        out=sums[j],
-                        lhsT=codes[:, slot, j * P : (j + 1) * P].bitcast(FP8X4),
-                        lhsT_scale=planes[:, slot, j * P : (j + 1) * P],
-                        rhs=w_codes[:, slot, :].bitcast(FP8X4),
-                        rhs_scale=w_planes[:, slot, :],
-                        start=(slot == QUANTISED_IN_ORDER[0]),
-                        stop=(slot == QUANTISED_IN_ORDER[-1]),
-                    )
+            first, last = QUANTISED_IN_ORDER[:-2], QUANTISED_IN_ORDER[-2:]
+            passes = [(slot, j) for slot in first for j in token_tiles]
+            passes += [(slot, j) for j in token_tiles for slot in last]
+            for slot, j in passes:
+                nc.tensor.matmul_mx(
+                    out=sums[j],
+                    lhsT=codes[:, slot, j * P : (j + 1) * P].bitcast(FP8X4),
+                    lhsT_scale=planes[:, slot, j * P : (j + 1) * P],
+                    rhs=w_codes[:, slot, :].bitcast(FP8X4),
+                    rhs_scale=w_planes[:, slot, :],
+                    start=(slot == QUANTISED_IN_ORDER[0]),
+                    stop=(slot == QUANTISED_IN_ORDER[-1]),
+                )
             return sums
 
         def finish(c, sums):
             for j in token_tiles:
                 first = c * CHUNK_ROWS + j * P
-                result = vector_out.tile([P, OUTPUTS], F32)
+                result = vector_out.tile([P, OUTPUTS], F32, bufs=4)
                 nc.vector.tensor_tensor(out=result, in0=sums[j], in1=bias_all, op=ALU.add)
                 nc.sync.dma_start(out=out_rows[first : first + P, :], in_=result)
 
-        made = scalar_part(0)
-        make_weights()
-        sums = None
+        bank = turn_x(0)
+        turn_sp(0)
+        away = distances(0, bank)
+        is_low = masks(0)
+        waiting = None
+        for a in range(OUTPUTS // P):
+            if a == 1:
+                words_bank = turn_x_words(0)
+                made = factors(away, words_bank)
+                turn_sp(1)
+            for h in range(NB // 2):
+                piece = weight_piece(a, h)
+                if waiting is not None:
+                    quantise_piece(*waiting)
+                waiting = piece
+        quantise_piece(*waiting)
+        before = None
         for c in range(CHUNKS):
-            ahead = scalar_part(c + 1) if c + 1 < CHUNKS else None
-            codes, planes = vector_part(c, *made)
-            if c > 0:
-                finish(c - 1, sums)
-            sums = multiply(codes, planes)
-            made = ahead
-        finish(CHUNKS - 1, sums)
+            if c + 1 < CHUNKS:
+                bank = turn_x(c + 1)
+                words_bank = turn_x_words(c + 1)
+                away = distances(c + 1, bank)
+                ahead = factors(away, words_bank)
+            codes, planes = vector_part(is_low, before, *made)
+            if c + 1 < CHUNKS:
+                is_low = masks(c + 1)
+                made = ahead
+            before = (c, multiply(codes, planes))
+        finish(*before)

@@ -26,6 +26,7 @@ HALF_ROWS = P // 2
 CHUNK_HALF_TILES = CHUNK_ROWS // HALF_ROWS
 CHUNK = CHUNK_ROWS * PACK
 CHUNKS = TOKENS // CHUNK_ROWS
+UNITS_FIRST = 7
 QUANTISED_IN_ORDER = (2, 3, NB, 0, 1, 4, 5)
 
 TAIL_SCALE = 6.0 ** -0.5
@@ -193,12 +194,6 @@ def tile_kanoriginal_kernel(
                 out=tail_squares[:, 2:4, :], in_=away[:, 2:4, :], func=ACT.Square,
                 bias=tail_bias, scale=TAIL_SCALE,
             )
-            silu = scalar_out.tile([P, CHUNK], BF16, align_bytes=64)
-            nc.scalar.activation(
-                out=silu.rearrange("p (r h e) -> p r h e", h=2, e=2),
-                in_=words_bank.bitcast(BF16).rearrange("p h (r e) -> p r h e", e=2),
-                func=ACT.Silu,
-            )
             to_odd = scalar_out.tile([P, CHUNK], F32)
             nc.scalar.activation(out=to_odd, in_=away[:, 0, :], func=ACT.Abs, bias=minus_one)
             nc.scalar.activation(
@@ -221,20 +216,16 @@ def tile_kanoriginal_kernel(
                 out=quad[:, 1, :], in_=to_odd, func=ACT.Square,
                 bias=quad_bias_odd, scale=CORE_SCALE,
             )
+            silu = scalar_out.tile([P, CHUNK], BF16, align_bytes=64)
+            nc.scalar.activation(
+                out=silu.rearrange("p (r h e) -> p r h e", h=2, e=2),
+                in_=words_bank.bitcast(BF16).rearrange("p h (r e) -> p r h e", e=2),
+                func=ACT.Silu,
+            )
             return silu, away, tail_squares, line, quad
 
-        def masks(c):
+        def vector_part(c, between, before, silu, away, tail_squares, line, quad):
             x_c = x_t[:, c * CHUNK : (c + 1) * CHUNK]
-            is_low = vector_own.tile([P, 2, CHUNK], BF16)
-            nc.vector.tensor_scalar(
-                out=is_low[:, 0, :], in0=x_c, scalar1=-1.0 / 3.0, scalar2=None, op0=ALU.is_lt
-            )
-            nc.vector.tensor_scalar(
-                out=is_low[:, 1, :], in0=x_c, scalar1=1.0 / 3.0, scalar2=None, op0=ALU.is_lt
-            )
-            return is_low
-
-        def vector_part(is_low, before, silu, away, tail_squares, line, quad):
             pairs, singles = slice(0, 2), slice(2, 4)
             codes = vector_out.tile([P, SLOTS, CHUNK_ROWS], U32, align_bytes=64)
             planes = vector_out.tile([P, SLOTS, CHUNK_ROWS], U8, align_bytes=64)
@@ -252,16 +243,24 @@ def tile_kanoriginal_kernel(
                     out=neg[:, kind, :], in0=away[:, kind, :], scalar=2.0,
                     in1=tail_squares[:, kind, :], op0=ALU.subtract, op1=ALU.mult,
                 )
+                between()
             if before is not None:
                 finish(*before)
             neg_core = vector_own.tile([P, 2, CHUNK], BF16)
             nc.vector.scalar_tensor_tensor(
                 out=neg_core, in0=quad, scalar=BETA / 2.0, in1=line, op0=ALU.add, op1=ALU.mult
             )
+            is_low = vector_own.tile([P, 2, CHUNK], BF16)
+            for i, point in enumerate((-1.0 / 3.0, 1.0 / 3.0)):
+                nc.vector.tensor_scalar(
+                    out=is_low[:, i, :], in0=x_c, scalar1=point, scalar2=None, op0=ALU.is_lt
+                )
+            between()
             for kind in (singles, pairs):
                 nc.vector.tensor_tensor(
                     out=neg[:, kind, :], in0=neg[:, kind, :], in1=neg_core, op=ALU.max
                 )
+                between()
             basis = vector_own.tile([P, NB, CHUNK], BF16, align_bytes=64)
             both = neg[:, pairs, :]
             for cut, kind in ((basis[:, 2:4, :], singles), (both, pairs)):
@@ -352,29 +351,29 @@ def tile_kanoriginal_kernel(
         bank = turn_x(0)
         turn_sp(0)
         away = distances(0, bank)
-        is_low = masks(0)
-        waiting = None
-        for a in range(OUTPUTS // P):
-            if a == 1:
+        units = [(a, h) for a in range(OUTPUTS // P) for h in range(NB // 2)]
+        waiting = []
+
+        def next_unit():
+            if units:
+                waiting.append(weight_piece(*units.pop(0)))
+            if len(waiting) > 1 or (waiting and not units):
+                quantise_piece(*waiting.pop(0))
+
+        for n in range(UNITS_FIRST):
+            if n == NB // 2:
                 words_bank = turn_x_words(0)
                 made = factors(away, words_bank)
                 turn_sp(1)
-            for h in range(NB // 2):
-                piece = weight_piece(a, h)
-                if waiting is not None:
-                    quantise_piece(*waiting)
-                waiting = piece
-        quantise_piece(*waiting)
+            next_unit()
         before = None
         for c in range(CHUNKS):
+            codes, planes = vector_part(c, next_unit, before, *made)
+            while units or waiting:
+                next_unit()
             if c + 1 < CHUNKS:
                 bank = turn_x(c + 1)
                 words_bank = turn_x_words(c + 1)
-                away = distances(c + 1, bank)
-                ahead = factors(away, words_bank)
-            codes, planes = vector_part(is_low, before, *made)
-            if c + 1 < CHUNKS:
-                is_low = masks(c + 1)
-                made = ahead
+                made = factors(distances(c + 1, bank), words_bank)
             before = (c, multiply(codes, planes))
         finish(*before)

@@ -19,14 +19,13 @@ FEATURES = 512
 OUTPUTS = 512
 NB = 6
 SLOTS = NB + 1
-CHUNK_TILES = 2
-CHUNK_ROWS = CHUNK_TILES * P
 HALF = FEATURES // 2
 HALF_ROWS = P // 2
-CHUNK_HALF_TILES = CHUNK_ROWS // HALF_ROWS
-CHUNK = CHUNK_ROWS * PACK
-CHUNKS = TOKENS // CHUNK_ROWS
-UNITS_FIRST = 7
+HALF_PACK = HALF_ROWS * PACK
+CHUNK_SIZES = (128, 256, 256, 256, 128)
+CHUNKS = [(sum(CHUNK_SIZES[:c]), rows) for c, rows in enumerate(CHUNK_SIZES)]
+SP_ROWS = 256
+UNITS_FIRST = 12
 QUANTISED_IN_ORDER = (2, 3, NB, 0, 1, 4, 5)
 
 TAIL_SCALE = 6.0 ** -0.5
@@ -79,39 +78,39 @@ def tile_kanoriginal_kernel(
                 out=out, in_=rows.rearrange("(a r) (u i) -> (r u) a i", r=HALF_ROWS, u=2)
             )
 
-        def load_x(c):
+        def load_x(first, rows):
             nc.sync.dma_start(
-                out=x_sb[:, c * CHUNK_TILES : (c + 1) * CHUNK_TILES, :],
-                in_=x_rows[c * CHUNK_ROWS : (c + 1) * CHUNK_ROWS, :].rearrange(
-                    "(a r) i -> r a i", r=P
-                ),
+                out=x_sb[:, first // P : (first + rows) // P, :],
+                in_=x_rows[first : first + rows, :].rearrange("(a r) i -> r a i", r=P),
             )
 
-        def load_x_halves(c):
+        def load_x_halves(first, rows):
             load_half_rows(
-                x_half_sb[:, c * CHUNK_HALF_TILES : (c + 1) * CHUNK_HALF_TILES, :],
-                x_rows[c * CHUNK_ROWS : (c + 1) * CHUNK_ROWS, :],
+                x_half_sb[:, first // HALF_ROWS : (first + rows) // HALF_ROWS, :],
+                x_rows[first : first + rows, :],
             )
 
-        def load_sp(c):
+        def load_sp(first):
             load_half_rows(
-                sp_sb[:, c * CHUNK_HALF_TILES : (c + 1) * CHUNK_HALF_TILES, :],
-                scale_sp[c * CHUNK_ROWS : (c + 1) * CHUNK_ROWS, :],
+                sp_sb[:, first // HALF_ROWS : (first + SP_ROWS) // HALF_ROWS, :],
+                scale_sp[first : first + SP_ROWS, :],
             )
 
         def load_coef(a):
             load_half_rows(coef_sb[:, 2 * a : 2 * a + 2, :], coef_rows[a * P : (a + 1) * P, :])
 
-        load_x_halves(0)
+        load_x_halves(*CHUNKS[0])
         load_sp(0)
         load_coef(0)
-        load_x(0)
-        load_sp(1)
+        load_x(*CHUNKS[0])
+        load_sp(SP_ROWS)
+        load_x_halves(*CHUNKS[1])
         for a in range(1, OUTPUTS // P):
             load_coef(a)
-        for c in range(1, CHUNKS):
-            load_x_halves(c)
-            load_x(c)
+        load_x(*CHUNKS[1])
+        for chunk in CHUNKS[2:]:
+            load_x_halves(*chunk)
+            load_x(*chunk)
         w_codes = keep.tile([P, SLOTS, OUTPUTS], U32, align_bytes=64)
         w_planes = keep.tile([P, SLOTS, OUTPUTS], U8, align_bytes=64)
         nc.sync.dma_start(
@@ -154,29 +153,30 @@ def tile_kanoriginal_kernel(
 
         x_t = keep.tile([P, TOKENS * PACK], BF16)
 
-        def turn_x(c):
-            bank = psum_turn.tile([P, CHUNK], BF16, tag="bank")
-            for a in range(CHUNK_HALF_TILES):
+        def turn_x(first, rows):
+            bank = psum_turn.tile([P, rows * PACK], BF16, tag="bank")
+            for a in range(rows // HALF_ROWS):
                 turn_half_rows(
                     nc,
-                    bank[:, a * HALF : (a + 1) * HALF],
-                    x_half_sb[:, c * CHUNK_HALF_TILES + a, :],
+                    bank[:, a * HALF_PACK : (a + 1) * HALF_PACK],
+                    x_half_sb[:, first // HALF_ROWS + a, :],
                     ident_bf,
                 )
             return bank
 
-        def turn_x_words(c):
-            bank = psum_turn.tile([P, 2, CHUNK_ROWS], F32, tag="bank")
-            for a in range(CHUNK_TILES):
-                words = x_sb[:, c * CHUNK_TILES + a, :].bitcast(F32)
+        def turn_x_words(first, rows):
+            bank = psum_turn.tile([P, 2, rows], F32, tag="bank")
+            for a in range(rows // P):
+                words = x_sb[:, first // P + a, :].bitcast(F32)
                 for h in range(2):
                     nc.tensor.transpose(bank[:, h, a * P : (a + 1) * P], words[:, h::2], ident)
             return bank
 
-        def distances(c, bank):
-            x_c = x_t[:, c * CHUNK : (c + 1) * CHUNK]
+        def distances(first, rows, bank):
+            width = rows * PACK
+            x_c = x_t[:, first * PACK : first * PACK + width]
             nc.scalar.copy(out=x_c, in_=bank)
-            away = scalar_out.tile([P, 4, CHUNK], F32)
+            away = scalar_out.tile([P, 4, width], F32)
             nc.scalar.activation(
                 out=away[:, 2, :], in_=x_c, func=ACT.Abs, bias=plus_half, scale=1.5
             )
@@ -188,20 +188,21 @@ def tile_kanoriginal_kernel(
             )
             return away
 
-        def factors(away, words_bank):
-            tail_squares = scalar_out.tile([P, 4, CHUNK], F32)
+        def factors(rows, away, words_bank):
+            width = rows * PACK
+            tail_squares = scalar_out.tile([P, 4, width], F32)
             nc.scalar.activation(
                 out=tail_squares[:, 2:4, :], in_=away[:, 2:4, :], func=ACT.Square,
                 bias=tail_bias, scale=TAIL_SCALE,
             )
-            to_odd = scalar_out.tile([P, CHUNK], F32)
+            to_odd = scalar_out.tile([P, width], F32)
             nc.scalar.activation(out=to_odd, in_=away[:, 0, :], func=ACT.Abs, bias=minus_one)
             nc.scalar.activation(
                 out=tail_squares[:, 0:2, :], in_=away[:, 0:2, :], func=ACT.Square,
                 bias=tail_bias, scale=TAIL_SCALE,
             )
-            line = scalar_out.tile([P, 2, CHUNK], F32, bufs=1)
-            quad = scalar_out.tile([P, 2, CHUNK], F32, bufs=1)
+            line = scalar_out.tile([P, 2, width], F32, bufs=1)
+            quad = scalar_out.tile([P, 2, width], F32, bufs=1)
             nc.scalar.activation(
                 out=line[:, 0, :], in_=to_odd, func=ACT.Identity, bias=line_bias_even
             )
@@ -216,7 +217,7 @@ def tile_kanoriginal_kernel(
                 out=quad[:, 1, :], in_=to_odd, func=ACT.Square,
                 bias=quad_bias_odd, scale=CORE_SCALE,
             )
-            silu = scalar_out.tile([P, CHUNK], BF16, align_bytes=64)
+            silu = scalar_out.tile([P, width], BF16, align_bytes=64)
             nc.scalar.activation(
                 out=silu.rearrange("p (r h e) -> p r h e", h=2, e=2),
                 in_=words_bank.bitcast(BF16).rearrange("p h (r e) -> p r h e", e=2),
@@ -224,11 +225,12 @@ def tile_kanoriginal_kernel(
             )
             return silu, away, tail_squares, line, quad
 
-        def vector_part(c, between, before, silu, away, tail_squares, line, quad):
-            x_c = x_t[:, c * CHUNK : (c + 1) * CHUNK]
+        def vector_part(first, rows, between, before, silu, away, tail_squares, line, quad):
+            width = rows * PACK
+            x_c = x_t[:, first * PACK : first * PACK + width]
             pairs, singles = slice(0, 2), slice(2, 4)
-            codes = vector_out.tile([P, SLOTS, CHUNK_ROWS], U32, align_bytes=64)
-            planes = vector_out.tile([P, SLOTS, CHUNK_ROWS], U8, align_bytes=64)
+            codes = vector_out.tile([P, SLOTS, rows], U32, align_bytes=64)
+            planes = vector_out.tile([P, SLOTS, rows], U8, align_bytes=64)
 
             def quantise(values, slots):
                 nc.vector.quantize_mx(
@@ -237,7 +239,7 @@ def tile_kanoriginal_kernel(
                     in_=values,
                 )
 
-            neg = vector_own.tile([P, 4, CHUNK], BF16)
+            neg = vector_own.tile([P, 4, width], BF16)
             for kind in (singles, pairs):
                 nc.vector.scalar_tensor_tensor(
                     out=neg[:, kind, :], in0=away[:, kind, :], scalar=2.0,
@@ -246,11 +248,11 @@ def tile_kanoriginal_kernel(
                 between()
             if before is not None:
                 finish(*before)
-            neg_core = vector_own.tile([P, 2, CHUNK], BF16)
+            neg_core = vector_own.tile([P, 2, width], BF16)
             nc.vector.scalar_tensor_tensor(
                 out=neg_core, in0=quad, scalar=BETA / 2.0, in1=line, op0=ALU.add, op1=ALU.mult
             )
-            is_low = vector_own.tile([P, 2, CHUNK], BF16)
+            is_low = vector_own.tile([P, 2, width], BF16)
             for i, point in enumerate((-1.0 / 3.0, 1.0 / 3.0)):
                 nc.vector.tensor_scalar(
                     out=is_low[:, i, :], in0=x_c, scalar1=point, scalar2=None, op0=ALU.is_lt
@@ -261,7 +263,7 @@ def tile_kanoriginal_kernel(
                     out=neg[:, kind, :], in0=neg[:, kind, :], in1=neg_core, op=ALU.max
                 )
                 between()
-            basis = vector_own.tile([P, NB, CHUNK], BF16, align_bytes=64)
+            basis = vector_own.tile([P, NB, width], BF16, align_bytes=64)
             both = neg[:, pairs, :]
             for cut, kind in ((basis[:, 2:4, :], singles), (both, pairs)):
                 nc.vector.tensor_scalar(
@@ -288,16 +290,18 @@ def tile_kanoriginal_kernel(
 
         sp_t = keep.tile([P, OUTPUTS * PACK], BF16)
 
-        def turn_sp(c):
-            bank = psum_turn.tile([P, CHUNK], BF16, tag="bank")
-            for a in range(CHUNK_HALF_TILES):
+        def turn_sp(first):
+            bank = psum_turn.tile([P, SP_ROWS * PACK], BF16, tag="bank")
+            for a in range(SP_ROWS // HALF_ROWS):
                 turn_half_rows(
                     nc,
-                    bank[:, a * HALF : (a + 1) * HALF],
-                    sp_sb[:, c * CHUNK_HALF_TILES + a, :],
+                    bank[:, a * HALF_PACK : (a + 1) * HALF_PACK],
+                    sp_sb[:, first // HALF_ROWS + a, :],
                     ident_bf,
                 )
-            nc.vector.tensor_copy(out=sp_t[:, c * CHUNK : (c + 1) * CHUNK], in_=bank)
+            nc.vector.tensor_copy(
+                out=sp_t[:, first * PACK : (first + SP_ROWS) * PACK], in_=bank
+            )
 
         def weight_piece(a, h):
             bank = psum_turn.tile([P, 2, P * PACK], BF16, tag="bank")
@@ -305,7 +309,7 @@ def tile_kanoriginal_kernel(
                 for half in range(2):
                     turn_half_rows(
                         nc,
-                        bank[:, b, half * HALF : (half + 1) * HALF],
+                        bank[:, b, half * HALF_PACK : (half + 1) * HALF_PACK],
                         coef_sb[:, 2 * a + half, :].rearrange("k (i b) -> k b i", b=NB)[
                             :, 2 * h + b, :
                         ],
@@ -322,13 +326,12 @@ def tile_kanoriginal_kernel(
             )
             return piece, a, h
 
-        token_tiles = range(CHUNK_TILES)
-
-        def multiply(codes, planes):
+        def multiply(rows, codes, planes):
+            token_tiles = range(rows // P)
             sums = [psum_sums.tile([P, OUTPUTS], F32, name="sum%d" % j) for j in token_tiles]
-            first, last = QUANTISED_IN_ORDER[:-2], QUANTISED_IN_ORDER[-2:]
-            passes = [(slot, j) for slot in first for j in token_tiles]
-            passes += [(slot, j) for j in token_tiles for slot in last]
+            early, late = QUANTISED_IN_ORDER[:-2], QUANTISED_IN_ORDER[-2:]
+            passes = [(slot, j) for slot in early for j in token_tiles]
+            passes += [(slot, j) for j in token_tiles for slot in late]
             for slot, j in passes:
                 nc.tensor.matmul_mx(
                     out=sums[j],
@@ -341,16 +344,19 @@ def tile_kanoriginal_kernel(
                 )
             return sums
 
-        def finish(c, sums):
-            for j in token_tiles:
-                first = c * CHUNK_ROWS + j * P
+        def finish(first, sums):
+            for j, total in enumerate(sums):
+                row = first + j * P
                 result = vector_out.tile([P, OUTPUTS], F32, bufs=4)
-                nc.vector.tensor_tensor(out=result, in0=sums[j], in1=bias_all, op=ALU.add)
-                nc.sync.dma_start(out=out_rows[first : first + P, :], in_=result)
+                nc.vector.tensor_tensor(out=result, in0=total, in1=bias_all, op=ALU.add)
+                nc.sync.dma_start(out=out_rows[row : row + P, :], in_=result)
 
-        bank = turn_x(0)
+        def scalar_part(first, rows, turned, turned_words):
+            return factors(rows, distances(first, rows, turned), turned_words)
+
+        turned = turn_x(*CHUNKS[0])
         turn_sp(0)
-        away = distances(0, bank)
+        away = distances(*CHUNKS[0], turned)
         units = [(a, h) for a in range(OUTPUTS // P) for h in range(NB // 2)]
         waiting = []
 
@@ -362,18 +368,23 @@ def tile_kanoriginal_kernel(
 
         for n in range(UNITS_FIRST):
             if n == NB // 2:
-                words_bank = turn_x_words(0)
-                made = factors(away, words_bank)
-                turn_sp(1)
+                turned_words = turn_x_words(*CHUNKS[0])
+                made = [factors(CHUNKS[0][1], away, turned_words)]
+                turn_sp(SP_ROWS)
             next_unit()
+        def turn_and_start(c):
+            chunk = CHUNKS[c]
+            turned = turn_x(*chunk)
+            turned_words = turn_x_words(*chunk)
+            made.append(scalar_part(*chunk, turned, turned_words))
+
+        turn_and_start(1)
         before = None
-        for c in range(CHUNKS):
-            codes, planes = vector_part(c, next_unit, before, *made)
+        for c, (first, rows) in enumerate(CHUNKS):
+            codes, planes = vector_part(first, rows, next_unit, before, *made.pop(0))
             while units or waiting:
                 next_unit()
-            if c + 1 < CHUNKS:
-                bank = turn_x(c + 1)
-                words_bank = turn_x_words(c + 1)
-                made = factors(distances(c + 1, bank), words_bank)
-            before = (c, multiply(codes, planes))
+            if c + 2 < len(CHUNKS):
+                turn_and_start(c + 2)
+            before = (first, multiply(rows, codes, planes))
         finish(*before)

@@ -22,10 +22,10 @@ SLOTS = NB + 1
 HALF = FEATURES // 2
 HALF_ROWS = P // 2
 HALF_PACK = HALF_ROWS * PACK
-CHUNK_SIZES = (128, 256, 256, 256, 128)
+CHUNK_SIZES = (256, 256, 256, 256)
 CHUNKS = [(sum(CHUNK_SIZES[:c]), rows) for c, rows in enumerate(CHUNK_SIZES)]
 SP_ROWS = 256
-UNITS_FIRST = 12
+UNITS_FIRST = 3
 QUANTISED_IN_ORDER = (2, 3, NB, 0, 1, 4, 5)
 
 TAIL_SCALE = 6.0 ** -0.5
@@ -104,10 +104,11 @@ def tile_kanoriginal_kernel(
         load_coef(0)
         load_x(*CHUNKS[0])
         load_sp(SP_ROWS)
+        load_coef(1)
         load_x_halves(*CHUNKS[1])
-        for a in range(1, OUTPUTS // P):
-            load_coef(a)
         load_x(*CHUNKS[1])
+        for a in range(2, OUTPUTS // P):
+            load_coef(a)
         for chunk in CHUNKS[2:]:
             load_x_halves(*chunk)
             load_x(*chunk)
@@ -252,6 +253,7 @@ def tile_kanoriginal_kernel(
             nc.vector.scalar_tensor_tensor(
                 out=neg_core, in0=quad, scalar=BETA / 2.0, in1=line, op0=ALU.add, op1=ALU.mult
             )
+            between()
             is_low = vector_own.tile([P, 2, width], BF16)
             for i, point in enumerate((-1.0 / 3.0, 1.0 / 3.0)):
                 nc.vector.tensor_scalar(
@@ -270,8 +272,10 @@ def tile_kanoriginal_kernel(
                     out=cut, in0=neg[:, kind, :], scalar1=-1.0, scalar2=0.0,
                     op0=ALU.mult, op1=ALU.max,
                 )
+                between()
             quantise(basis[:, 2:4, :].rearrange("p s m -> p (s m)"), slice(2, 4))
             nc.vector.tensor_tensor(out=basis[:, 0:2, :], in0=both, in1=is_low, op=ALU.mult)
+            between()
             quantise(silu, slice(NB, SLOTS))
             nc.vector.tensor_tensor(
                 out=basis[:, 4:6, :], in0=both, in1=basis[:, 0:2, :], op=ALU.subtract
@@ -351,9 +355,6 @@ def tile_kanoriginal_kernel(
                 nc.vector.tensor_tensor(out=result, in0=total, in1=bias_all, op=ALU.add)
                 nc.sync.dma_start(out=out_rows[row : row + P, :], in_=result)
 
-        def scalar_part(first, rows, turned, turned_words):
-            return factors(rows, distances(first, rows, turned), turned_words)
-
         turned = turn_x(*CHUNKS[0])
         turn_sp(0)
         away = distances(*CHUNKS[0], turned)
@@ -367,24 +368,24 @@ def tile_kanoriginal_kernel(
                 quantise_piece(*waiting.pop(0))
 
         for n in range(UNITS_FIRST):
-            if n == NB // 2:
-                turned_words = turn_x_words(*CHUNKS[0])
-                made = [factors(CHUNKS[0][1], away, turned_words)]
-                turn_sp(SP_ROWS)
             next_unit()
-        def turn_and_start(c):
-            chunk = CHUNKS[c]
-            turned = turn_x(*chunk)
-            turned_words = turn_x_words(*chunk)
-            made.append(scalar_part(*chunk, turned, turned_words))
+        turned_words = turn_x_words(*CHUNKS[0])
+        made = factors(CHUNKS[0][1], away, turned_words)
+        turn_sp(SP_ROWS)
 
-        turn_and_start(1)
+        def turn_chunk(c):
+            return (turn_x(*CHUNKS[c]), turn_x_words(*CHUNKS[c])) if c < len(CHUNKS) else None
+
+        turned = turn_chunk(1)
         before = None
         for c, (first, rows) in enumerate(CHUNKS):
-            codes, planes = vector_part(first, rows, next_unit, before, *made.pop(0))
+            codes, planes = vector_part(first, rows, next_unit, before, *made)
             while units or waiting:
                 next_unit()
-            if c + 2 < len(CHUNKS):
-                turn_and_start(c + 2)
+            if turned is not None:
+                bank, words_bank = turned
+                away = distances(*CHUNKS[c + 1], bank)
+                made = factors(CHUNKS[c + 1][1], away, words_bank)
+                turned = turn_chunk(c + 2)
             before = (first, multiply(rows, codes, planes))
         finish(*before)

@@ -62,7 +62,7 @@ def tile_kanoriginal_kernel(
         scalar_out = ctx.enter_context(tc.tile_pool(name="scalar_out", bufs=2))
         vector_own = ctx.enter_context(tc.tile_pool(name="vector_own", bufs=1))
         vector_out = ctx.enter_context(tc.tile_pool(name="vector_out", bufs=2))
-        psum_turn = ctx.enter_context(tc.psum_pool(name="psum_turn", bufs=6))
+        psum_turn = ctx.enter_context(tc.psum_pool(name="psum_turn", bufs=3))
         psum_sums = ctx.enter_context(tc.psum_pool(name="psum_sums", bufs=1))
 
         ctx.enter_context(tc.manual_schedule())
@@ -155,7 +155,7 @@ def tile_kanoriginal_kernel(
         x_t = keep.tile([P, TOKENS * PACK], BF16)
 
         def turn_x(first, rows):
-            bank = psum_turn.tile([P, rows * PACK], BF16, tag="bank")
+            bank = psum_turn.tile([P, rows * PACK], BF16, tag="x", bufs=1)
             for a in range(rows // HALF_ROWS):
                 turn_half_rows(
                     nc,
@@ -166,36 +166,33 @@ def tile_kanoriginal_kernel(
             return bank
 
         def turn_x_words(first, rows):
-            bank = psum_turn.tile([P, 2, rows], F32, tag="bank")
+            bank = psum_turn.tile([P, 2, rows], F32, tag="words", bufs=2)
             for a in range(rows // P):
                 words = x_sb[:, first // P + a, :].bitcast(F32)
                 for h in range(2):
                     nc.tensor.transpose(bank[:, h, a * P : (a + 1) * P], words[:, h::2], ident)
             return bank
 
-        def distances(first, rows, bank):
+        def scalar_part(first, rows, bank, words_bank):
             width = rows * PACK
-            x_c = x_t[:, first * PACK : first * PACK + width]
-            nc.scalar.copy(out=x_c, in_=bank)
             away = scalar_out.tile([P, 4, width], F32)
             nc.scalar.activation(
-                out=away[:, 2, :], in_=x_c, func=ACT.Abs, bias=plus_half, scale=1.5
+                out=away[:, 2, :], in_=bank, func=ACT.Abs, bias=plus_half, scale=1.5
             )
             nc.scalar.activation(
-                out=away[:, 3, :], in_=x_c, func=ACT.Abs, bias=minus_half, scale=1.5
+                out=away[:, 3, :], in_=bank, func=ACT.Abs, bias=minus_half, scale=1.5
             )
-            nc.scalar.activation(
-                out=away[:, 0:2, :], in_=away[:, 2:4, :], func=ACT.Abs, bias=minus_two
-            )
-            return away
-
-        def factors(rows, away, words_bank):
-            width = rows * PACK
+            x_c = x_t[:, first * PACK : first * PACK + width]
+            nc.scalar.copy(out=x_c, in_=bank)
             tail_squares = scalar_out.tile([P, 4, width], F32)
             nc.scalar.activation(
                 out=tail_squares[:, 2:4, :], in_=away[:, 2:4, :], func=ACT.Square,
                 bias=tail_bias, scale=TAIL_SCALE,
             )
+            for i in range(2):
+                nc.scalar.activation(
+                    out=away[:, i, :], in_=away[:, 2 + i, :], func=ACT.Abs, bias=minus_two
+                )
             to_odd = scalar_out.tile([P, width], F32)
             nc.scalar.activation(out=to_odd, in_=away[:, 0, :], func=ACT.Abs, bias=minus_one)
             nc.scalar.activation(
@@ -357,7 +354,6 @@ def tile_kanoriginal_kernel(
 
         turned = turn_x(*CHUNKS[0])
         turn_sp(0)
-        away = distances(*CHUNKS[0], turned)
         units = [(a, h) for a in range(OUTPUTS // P) for h in range(NB // 2)]
         waiting = []
 
@@ -370,7 +366,7 @@ def tile_kanoriginal_kernel(
         for n in range(UNITS_FIRST):
             next_unit()
         turned_words = turn_x_words(*CHUNKS[0])
-        made = factors(CHUNKS[0][1], away, turned_words)
+        made = scalar_part(*CHUNKS[0], turned, turned_words)
         turn_sp(SP_ROWS)
 
         def turn_chunk(c):
@@ -383,9 +379,7 @@ def tile_kanoriginal_kernel(
             while units or waiting:
                 next_unit()
             if turned is not None:
-                bank, words_bank = turned
-                away = distances(*CHUNKS[c + 1], bank)
-                made = factors(CHUNKS[c + 1][1], away, words_bank)
+                made = scalar_part(*CHUNKS[c + 1], *turned)
                 turned = turn_chunk(c + 2)
             before = (first, multiply(rows, codes, planes))
         finish(*before)

@@ -45,7 +45,7 @@ def turn_half_rows(nc, out, half_rows, ident):
     for e in range(2):
         nc.tensor.transpose(
             out.rearrange("p (r e u) -> p e r u", e=2, u=2)[:, e],
-            half_rows.rearrange("k (p e) -> k e p", e=2)[:, e, :],
+            half_rows[:, e * P : (e + 1) * P],
             ident,
         )
 

@@ -22,10 +22,11 @@ SLOTS = NB + 1
 HALF = FEATURES // 2
 HALF_ROWS = P // 2
 HALF_PACK = HALF_ROWS * PACK
-CHUNK_SIZES = (256, 256, 256, 256)
+CHUNK_SIZES = (128, 256, 256, 256, 128)
 CHUNKS = [(sum(CHUNK_SIZES[:c]), rows) for c, rows in enumerate(CHUNK_SIZES)]
 SP_ROWS = 256
 UNITS_FIRST = 3
+UNITS_BETWEEN = {0: (1, 2), 1: (3, 3)}
 QUANTISED_IN_ORDER = (2, 3, NB, 0, 1, 4, 5)
 
 TAIL_SCALE = 6.0 ** -0.5
@@ -63,7 +64,7 @@ def tile_kanoriginal_kernel(
         vector_own = ctx.enter_context(tc.tile_pool(name="vector_own", bufs=1))
         vector_out = ctx.enter_context(tc.tile_pool(name="vector_out", bufs=2))
         psum_turn = ctx.enter_context(tc.psum_pool(name="psum_turn", bufs=3))
-        psum_sums = ctx.enter_context(tc.psum_pool(name="psum_sums", bufs=1))
+        psum_sums = ctx.enter_context(tc.psum_pool(name="psum_sums", bufs=3))
 
         ctx.enter_context(tc.manual_schedule())
 
@@ -103,9 +104,9 @@ def tile_kanoriginal_kernel(
         load_sp(0)
         load_coef(0)
         load_x(*CHUNKS[0])
+        load_x_halves(*CHUNKS[1])
         load_sp(SP_ROWS)
         load_coef(1)
-        load_x_halves(*CHUNKS[1])
         load_x(*CHUNKS[1])
         for a in range(2, OUTPUTS // P):
             load_coef(a)
@@ -166,7 +167,7 @@ def tile_kanoriginal_kernel(
             return bank
 
         def turn_x_words(first, rows):
-            bank = psum_turn.tile([P, 2, rows], F32, tag="words", bufs=2)
+            bank = psum_turn.tile([P, 2, rows], F32, tag="words", bufs=1)
             for a in range(rows // P):
                 words = x_sb[:, first // P + a, :].bitcast(F32)
                 for h in range(2):
@@ -223,7 +224,16 @@ def tile_kanoriginal_kernel(
             )
             return silu, away, tail_squares, line, quad
 
-        def vector_part(first, rows, between, before, silu, away, tail_squares, line, quad):
+        units = [(a, h) for a in range(OUTPUTS // P) for h in range(NB // 2)]
+        waiting = []
+
+        def next_unit():
+            if units:
+                waiting.append(weight_piece(*units.pop(0)))
+            if len(waiting) > 1 or (waiting and not units):
+                quantise_piece(*waiting.pop(0))
+
+        def vector_part(first, rows, units_between, unfinished, silu, away, tail_squares, line, quad):
             width = rows * PACK
             x_c = x_t[:, first * PACK : first * PACK + width]
             pairs, singles = slice(0, 2), slice(2, 4)
@@ -238,30 +248,35 @@ def tile_kanoriginal_kernel(
                 )
 
             neg = vector_own.tile([P, 4, width], BF16)
-            for kind in (singles, pairs):
+            for kind, count in zip((singles, pairs), units_between):
                 nc.vector.scalar_tensor_tensor(
                     out=neg[:, kind, :], in0=away[:, kind, :], scalar=2.0,
                     in1=tail_squares[:, kind, :], op0=ALU.subtract, op1=ALU.mult,
                 )
-                between()
-            if before is not None:
-                finish(*before)
+                for n in range(count):
+                    next_unit()
+            is_low = vector_own.tile([P, 2, width], BF16)
+
+            def mask(i, point):
+                nc.vector.tensor_scalar(
+                    out=is_low[:, i, :], in0=x_c, scalar1=point, scalar2=None, op0=ALU.is_lt
+                )
+
+            mask(0, -1.0 / 3.0)
+            while unfinished:
+                finish(*unfinished.pop(0))
             neg_core = vector_own.tile([P, 2, width], BF16)
             nc.vector.scalar_tensor_tensor(
                 out=neg_core, in0=quad, scalar=BETA / 2.0, in1=line, op0=ALU.add, op1=ALU.mult
             )
-            between()
-            is_low = vector_own.tile([P, 2, width], BF16)
-            for i, point in enumerate((-1.0 / 3.0, 1.0 / 3.0)):
-                nc.vector.tensor_scalar(
-                    out=is_low[:, i, :], in0=x_c, scalar1=point, scalar2=None, op0=ALU.is_lt
-                )
-            between()
+            mask(1, 1.0 / 3.0)
+            if not units:
+                while waiting:
+                    next_unit()
             for kind in (singles, pairs):
                 nc.vector.tensor_tensor(
                     out=neg[:, kind, :], in0=neg[:, kind, :], in1=neg_core, op=ALU.max
                 )
-                between()
             basis = vector_own.tile([P, NB, width], BF16, align_bytes=64)
             both = neg[:, pairs, :]
             for cut, kind in ((basis[:, 2:4, :], singles), (both, pairs)):
@@ -269,10 +284,8 @@ def tile_kanoriginal_kernel(
                     out=cut, in0=neg[:, kind, :], scalar1=-1.0, scalar2=0.0,
                     op0=ALU.mult, op1=ALU.max,
                 )
-                between()
             quantise(basis[:, 2:4, :].rearrange("p s m -> p (s m)"), slice(2, 4))
             nc.vector.tensor_tensor(out=basis[:, 0:2, :], in0=both, in1=is_low, op=ALU.mult)
-            between()
             quantise(silu, slice(NB, SLOTS))
             nc.vector.tensor_tensor(
                 out=basis[:, 4:6, :], in0=both, in1=basis[:, 0:2, :], op=ALU.subtract
@@ -329,7 +342,7 @@ def tile_kanoriginal_kernel(
 
         def multiply(rows, codes, planes):
             token_tiles = range(rows // P)
-            sums = [psum_sums.tile([P, OUTPUTS], F32, name="sum%d" % j) for j in token_tiles]
+            sums = [psum_sums.tile([P, OUTPUTS], F32, name="sum") for j in token_tiles]
             early, late = QUANTISED_IN_ORDER[:-2], QUANTISED_IN_ORDER[-2:]
             passes = [(slot, j) for slot in early for j in token_tiles]
             passes += [(slot, j) for j in token_tiles for slot in late]
@@ -352,34 +365,27 @@ def tile_kanoriginal_kernel(
                 nc.vector.tensor_tensor(out=result, in0=total, in1=bias_all, op=ALU.add)
                 nc.sync.dma_start(out=out_rows[row : row + P, :], in_=result)
 
-        turned = turn_x(*CHUNKS[0])
+        bank = turn_x(*CHUNKS[0])
         turn_sp(0)
-        units = [(a, h) for a in range(OUTPUTS // P) for h in range(NB // 2)]
-        waiting = []
-
-        def next_unit():
-            if units:
-                waiting.append(weight_piece(*units.pop(0)))
-            if len(waiting) > 1 or (waiting and not units):
-                quantise_piece(*waiting.pop(0))
-
         for n in range(UNITS_FIRST):
             next_unit()
-        turned_words = turn_x_words(*CHUNKS[0])
-        made = scalar_part(*CHUNKS[0], turned, turned_words)
+        made = scalar_part(*CHUNKS[0], bank, turn_x_words(*CHUNKS[0]))
         turn_sp(SP_ROWS)
-
-        def turn_chunk(c):
-            return (turn_x(*CHUNKS[c]), turn_x_words(*CHUNKS[c])) if c < len(CHUNKS) else None
-
-        turned = turn_chunk(1)
-        before = None
+        bank = turn_x(*CHUNKS[1])
+        quantised = []
+        unfinished = []
         for c, (first, rows) in enumerate(CHUNKS):
-            codes, planes = vector_part(first, rows, next_unit, before, *made)
-            while units or waiting:
-                next_unit()
-            if turned is not None:
-                made = scalar_part(*CHUNKS[c + 1], *turned)
-                turned = turn_chunk(c + 2)
-            before = (first, multiply(rows, codes, planes))
-        finish(*before)
+            codes, planes = vector_part(
+                first, rows, UNITS_BETWEEN.get(c, (0, 0)), unfinished, *made
+            )
+            quantised.append((first, rows, codes, planes))
+            if c + 1 < len(CHUNKS):
+                made = scalar_part(*CHUNKS[c + 1], bank, turn_x_words(*CHUNKS[c + 1]))
+            if c + 2 < len(CHUNKS):
+                bank = turn_x(*CHUNKS[c + 2])
+            if c > 0:
+                while quantised:
+                    first, rows, codes, planes = quantised.pop(0)
+                    unfinished.append((first, multiply(rows, codes, planes)))
+        while unfinished:
+            finish(*unfinished.pop(0))

@@ -24,9 +24,10 @@ HALF_ROWS = P // 2
 HALF_PACK = HALF_ROWS * PACK
 CHUNK_SIZES = (128, 256, 256, 256, 128)
 CHUNKS = [(sum(CHUNK_SIZES[:c]), rows) for c, rows in enumerate(CHUNK_SIZES)]
-SP_ROWS = 256
-UNITS_FIRST = 3
-UNITS_BETWEEN = {0: (1, 2), 1: (3, 3)}
+LATE_FROM = 640
+SPLITS = (-1.0 / 3.0, 1.0 / 3.0)
+UNITS_FIRST = 4
+UNITS_BETWEEN = {0: (1, 2), 1: (3, 2)}
 QUANTISED_IN_ORDER = (2, 3, NB, 0, 1, 4, 5)
 
 TAIL_SCALE = 6.0 ** -0.5
@@ -63,8 +64,7 @@ def tile_kanoriginal_kernel(
         scalar_out = ctx.enter_context(tc.tile_pool(name="scalar_out", bufs=2))
         vector_own = ctx.enter_context(tc.tile_pool(name="vector_own", bufs=1))
         vector_out = ctx.enter_context(tc.tile_pool(name="vector_out", bufs=2))
-        psum_turn = ctx.enter_context(tc.psum_pool(name="psum_turn", bufs=3))
-        psum_sums = ctx.enter_context(tc.psum_pool(name="psum_sums", bufs=3))
+        psum = ctx.enter_context(tc.psum_pool(name="psum", bufs=5))
 
         ctx.enter_context(tc.manual_schedule())
 
@@ -91,25 +91,29 @@ def tile_kanoriginal_kernel(
                 x_rows[first : first + rows, :],
             )
 
-        def load_sp(first):
+        def load_sp(first, rows):
             load_half_rows(
-                sp_sb[:, first // HALF_ROWS : (first + SP_ROWS) // HALF_ROWS, :],
-                scale_sp[first : first + SP_ROWS, :],
+                sp_sb[:, first // HALF_ROWS : (first + rows) // HALF_ROWS, :],
+                scale_sp[first : first + rows, :],
             )
 
-        def load_coef(a):
-            load_half_rows(coef_sb[:, 2 * a : 2 * a + 2, :], coef_rows[a * P : (a + 1) * P, :])
+        def load_coef(first, rows):
+            load_half_rows(
+                coef_sb[:, first // HALF_ROWS : (first + rows) // HALF_ROWS, :],
+                coef_rows[first : first + rows, :],
+            )
 
         load_x_halves(*CHUNKS[0])
-        load_sp(0)
-        load_coef(0)
+        load_sp(0, P)
+        load_coef(0, HALF_ROWS)
+        load_coef(HALF_ROWS, HALF_ROWS)
         load_x(*CHUNKS[0])
+        load_sp(P, OUTPUTS - P)
         load_x_halves(*CHUNKS[1])
-        load_sp(SP_ROWS)
-        load_coef(1)
+        load_coef(P, P)
         load_x(*CHUNKS[1])
         for a in range(2, OUTPUTS // P):
-            load_coef(a)
+            load_coef(a * P, P)
         for chunk in CHUNKS[2:]:
             load_x_halves(*chunk)
             load_x(*chunk)
@@ -147,6 +151,9 @@ def tile_kanoriginal_kernel(
         minus_half = bias_column("minus_half", -0.5)
         minus_one = bias_column("minus_one", -1.0)
         minus_two = bias_column("minus_two", -2.0)
+        split_columns = [
+            bias_column("split_%d" % i, -split) for i, split in enumerate(SPLITS)
+        ]
         tail_bias = bias_column("tail_bias", -2.0 * TAIL_SCALE)
         line_bias_even = bias_column("line_bias_even", -(1.0 + RHO))
         line_bias_odd = bias_column("line_bias_odd", -RHO)
@@ -156,7 +163,7 @@ def tile_kanoriginal_kernel(
         x_t = keep.tile([P, TOKENS * PACK], BF16)
 
         def turn_x(first, rows):
-            bank = psum_turn.tile([P, rows * PACK], BF16, tag="x", bufs=1)
+            bank = psum.tile([P, rows * PACK], BF16, tag="x", bufs=2)
             for a in range(rows // HALF_ROWS):
                 turn_half_rows(
                     nc,
@@ -167,7 +174,7 @@ def tile_kanoriginal_kernel(
             return bank
 
         def turn_x_words(first, rows):
-            bank = psum_turn.tile([P, 2, rows], F32, tag="words", bufs=1)
+            bank = psum.tile([P, 2, rows], F32, tag="words", bufs=1)
             for a in range(rows // P):
                 words = x_sb[:, first // P + a, :].bitcast(F32)
                 for h in range(2):
@@ -184,7 +191,8 @@ def tile_kanoriginal_kernel(
                 out=away[:, 3, :], in_=bank, func=ACT.Abs, bias=minus_half, scale=1.5
             )
             x_c = x_t[:, first * PACK : first * PACK + width]
-            nc.scalar.copy(out=x_c, in_=bank)
+            if first < LATE_FROM:
+                nc.scalar.copy(out=x_c, in_=bank)
             tail_squares = scalar_out.tile([P, 4, width], F32)
             nc.scalar.activation(
                 out=tail_squares[:, 2:4, :], in_=away[:, 2:4, :], func=ACT.Square,
@@ -222,21 +230,38 @@ def tile_kanoriginal_kernel(
                 in_=words_bank.bitcast(BF16).rearrange("p h (r e) -> p r h e", e=2),
                 func=ACT.Silu,
             )
-            return silu, away, tail_squares, line, quad
+            side = None
+            if first >= LATE_FROM:
+                side = scalar_out.tile([P, 2, width], BF16)
+                for i, column in enumerate(split_columns):
+                    nc.scalar.activation(out=side[:, i, :], in_=bank, func=ACT.Sign, bias=column)
+            return silu, away, tail_squares, line, quad, side
 
         units = [(a, h) for a in range(OUTPUTS // P) for h in range(NB // 2)]
         waiting = []
 
         def next_unit():
             if units:
-                waiting.append(weight_piece(*units.pop(0)))
+                a, h = units.pop(0)
+                waiting.append(weight_piece(a, h))
+                if h == 0 and a + 1 < OUTPUTS // P:
+                    turn_sp(a + 1)
             if len(waiting) > 1 or (waiting and not units):
                 quantise_piece(*waiting.pop(0))
 
-        def vector_part(first, rows, units_between, unfinished, silu, away, tail_squares, line, quad):
+        def vector_part(
+            first, rows, units_between, unfinished, silu, away, tail_squares, line, quad, side
+        ):
             width = rows * PACK
             x_c = x_t[:, first * PACK : first * PACK + width]
             pairs, singles = slice(0, 2), slice(2, 4)
+
+            def make_side(side, i):
+                nc.vector.tensor_scalar(
+                    out=side[:, i, :], in0=x_c, scalar1=SPLITS[i], scalar2=0.5,
+                    op0=ALU.is_ge, op1=ALU.subtract,
+                )
+
             codes = vector_out.tile([P, SLOTS, rows], U32, align_bytes=64)
             planes = vector_out.tile([P, SLOTS, rows], U8, align_bytes=64)
 
@@ -255,21 +280,19 @@ def tile_kanoriginal_kernel(
                 )
                 for n in range(count):
                     next_unit()
-            is_low = vector_own.tile([P, 2, width], BF16)
-
-            def mask(i, point):
-                nc.vector.tensor_scalar(
-                    out=is_low[:, i, :], in0=x_c, scalar1=point, scalar2=None, op0=ALU.is_lt
-                )
-
-            mask(0, -1.0 / 3.0)
-            while unfinished:
-                finish(*unfinished.pop(0))
+            side_scale = 1.0
+            if side is None:
+                side = vector_own.tile([P, 2, width], BF16)
+                side_scale = 0.5
+                make_side(side, 0)
             neg_core = vector_own.tile([P, 2, width], BF16)
             nc.vector.scalar_tensor_tensor(
                 out=neg_core, in0=quad, scalar=BETA / 2.0, in1=line, op0=ALU.add, op1=ALU.mult
             )
-            mask(1, 1.0 / 3.0)
+            if side_scale == 0.5:
+                make_side(side, 1)
+            while unfinished:
+                finish(*unfinished.pop(0))
             if not units:
                 while waiting:
                     next_unit()
@@ -279,17 +302,21 @@ def tile_kanoriginal_kernel(
                 )
             basis = vector_own.tile([P, NB, width], BF16, align_bytes=64)
             both = neg[:, pairs, :]
-            for cut, kind in ((basis[:, 2:4, :], singles), (both, pairs)):
-                nc.vector.tensor_scalar(
-                    out=cut, in0=neg[:, kind, :], scalar1=-1.0, scalar2=0.0,
-                    op0=ALU.mult, op1=ALU.max,
-                )
-            quantise(basis[:, 2:4, :].rearrange("p s m -> p (s m)"), slice(2, 4))
-            nc.vector.tensor_tensor(out=basis[:, 0:2, :], in0=both, in1=is_low, op=ALU.mult)
-            quantise(silu, slice(NB, SLOTS))
-            nc.vector.tensor_tensor(
-                out=basis[:, 4:6, :], in0=both, in1=basis[:, 0:2, :], op=ALU.subtract
+            nc.vector.tensor_scalar(
+                out=basis[:, 2:4, :], in0=neg[:, singles, :], scalar1=-1.0, scalar2=0.0,
+                op0=ALU.mult, op1=ALU.max,
             )
+            nc.vector.tensor_scalar(
+                out=both, in0=both, scalar1=0.0, scalar2=None, op0=ALU.min
+            )
+            quantise(basis[:, 2:4, :].rearrange("p s m -> p (s m)"), slice(2, 4))
+            nc.vector.tensor_tensor(out=both, in0=both, in1=side, op=ALU.mult)
+            quantise(silu, slice(NB, SLOTS))
+            for low, sign in ((0, 1.0), (4, -1.0)):
+                nc.vector.tensor_scalar(
+                    out=basis[:, low : low + 2, :], in0=both, scalar1=sign / side_scale,
+                    scalar2=0.0, op0=ALU.mult, op1=ALU.max,
+                )
             quantise(basis[:, 0:2, :].rearrange("p s m -> p (s m)"), slice(0, 2))
             quantise(basis[:, 4:6, :].rearrange("p s m -> p (s m)"), slice(4, 6))
             return codes, planes
@@ -304,23 +331,21 @@ def tile_kanoriginal_kernel(
 
         sp_t = keep.tile([P, OUTPUTS * PACK], BF16)
 
-        def turn_sp(first):
-            bank = psum_turn.tile([P, SP_ROWS * PACK], BF16, tag="bank")
-            for a in range(SP_ROWS // HALF_ROWS):
+        def turn_sp(a):
+            bank = psum.tile([P, P * PACK], BF16, tag="bank")
+            for half in range(2):
                 turn_half_rows(
                     nc,
-                    bank[:, a * HALF_PACK : (a + 1) * HALF_PACK],
-                    sp_sb[:, first // HALF_ROWS + a, :],
+                    bank[:, half * HALF_PACK : (half + 1) * HALF_PACK],
+                    sp_sb[:, 2 * a + half, :],
                     ident_bf,
                 )
-            nc.vector.tensor_copy(
-                out=sp_t[:, first * PACK : (first + SP_ROWS) * PACK], in_=bank
-            )
+            nc.vector.tensor_copy(out=sp_t[:, a * P * PACK : (a + 1) * P * PACK], in_=bank)
 
         def weight_piece(a, h):
-            bank = psum_turn.tile([P, 2, P * PACK], BF16, tag="bank")
-            for b in range(2):
-                for half in range(2):
+            bank = psum.tile([P, 2, P * PACK], BF16, tag="bank")
+            for half in range(2):
+                for b in range(2):
                     turn_half_rows(
                         nc,
                         bank[:, b, half * HALF_PACK : (half + 1) * HALF_PACK],
@@ -340,37 +365,44 @@ def tile_kanoriginal_kernel(
             )
             return piece, a, h
 
-        def multiply(rows, codes, planes):
-            token_tiles = range(rows // P)
-            sums = [psum_sums.tile([P, OUTPUTS], F32, name="sum") for j in token_tiles]
+        def multiply(rows, codes, planes, last_chunk):
+            halves = [slice(0, OUTPUTS // 2), slice(OUTPUTS // 2, OUTPUTS)]
+            columns = halves if last_chunk else [slice(0, OUTPUTS)]
+            parts = [(j, cols) for j in range(rows // P) for cols in columns]
+            sums = []
+            for j, cols in parts:
+                total = psum.tile([P, OUTPUTS], F32, tag="bank", name="sum")
+                sums.append((j * P, cols, total[:, cols]))
             early, late = QUANTISED_IN_ORDER[:-2], QUANTISED_IN_ORDER[-2:]
-            passes = [(slot, j) for slot in early for j in token_tiles]
-            passes += [(slot, j) for j in token_tiles for slot in late]
-            for slot, j in passes:
+            passes = [(slot, n) for slot in early for n in range(len(parts))]
+            passes += [(slot, n) for n in range(len(parts)) for slot in late]
+            for slot, n in passes:
+                j, cols = parts[n]
                 nc.tensor.matmul_mx(
-                    out=sums[j],
+                    out=sums[n][2],
                     lhsT=codes[:, slot, j * P : (j + 1) * P].bitcast(FP8X4),
                     lhsT_scale=planes[:, slot, j * P : (j + 1) * P],
-                    rhs=w_codes[:, slot, :].bitcast(FP8X4),
-                    rhs_scale=w_planes[:, slot, :],
+                    rhs=w_codes[:, slot, cols].bitcast(FP8X4),
+                    rhs_scale=w_planes[:, slot, cols],
                     start=(slot == QUANTISED_IN_ORDER[0]),
                     stop=(slot == QUANTISED_IN_ORDER[-1]),
                 )
             return sums
 
         def finish(first, sums):
-            for j, total in enumerate(sums):
-                row = first + j * P
+            for offset, cols, total in sums:
+                row = first + offset
                 result = vector_out.tile([P, OUTPUTS], F32, bufs=4)
-                nc.vector.tensor_tensor(out=result, in0=total, in1=bias_all, op=ALU.add)
-                nc.sync.dma_start(out=out_rows[row : row + P, :], in_=result)
+                nc.vector.tensor_tensor(
+                    out=result[:, cols], in0=total, in1=bias_all[:, cols], op=ALU.add
+                )
+                nc.sync.dma_start(out=out_rows[row : row + P, cols], in_=result[:, cols])
 
         bank = turn_x(*CHUNKS[0])
         turn_sp(0)
         for n in range(UNITS_FIRST):
             next_unit()
         made = scalar_part(*CHUNKS[0], bank, turn_x_words(*CHUNKS[0]))
-        turn_sp(SP_ROWS)
         bank = turn_x(*CHUNKS[1])
         quantised = []
         unfinished = []
@@ -386,6 +418,6 @@ def tile_kanoriginal_kernel(
             if c > 0:
                 while quantised:
                     first, rows, codes, planes = quantised.pop(0)
-                    unfinished.append((first, multiply(rows, codes, planes)))
+                    unfinished.append((first, multiply(rows, codes, planes, c + 1 == len(CHUNKS))))
         while unfinished:
             finish(*unfinished.pop(0))

@@ -22,12 +22,12 @@ SLOTS = NB + 1
 HALF = FEATURES // 2
 HALF_ROWS = P // 2
 HALF_PACK = HALF_ROWS * PACK
-CHUNK_SIZES = (128, 256, 256, 256, 128)
+CHUNK_SIZES = (256, 256, 256, 256)
 CHUNKS = [(sum(CHUNK_SIZES[:c]), rows) for c, rows in enumerate(CHUNK_SIZES)]
-LATE_FROM = 640
+LATE_FROM = 768
 SPLITS = (-1.0 / 3.0, 1.0 / 3.0)
 UNITS_FIRST = 4
-UNITS_BETWEEN = {0: (1, 2), 1: (3, 2)}
+UNITS_BETWEEN = {0: (3, 2), 1: (2, 1)}
 QUANTISED_IN_ORDER = (2, 3, NB, 0, 1, 4, 5)
 
 TAIL_SCALE = 6.0 ** -0.5
@@ -139,6 +139,9 @@ def tile_kanoriginal_kernel(
         make_identity(nc, ident)
         one = keep.tile([P, 1], F32)
         nc.vector.memset(one, 1.0)
+
+        warm = keep.tile([P, 1], F32)
+        nc.scalar.activation(out=warm, in_=one, func=ACT.Silu)
 
         def bias_column(name, value):
             column = keep.tile([P, 1], F32, name=name)

@@ -24,10 +24,10 @@ HALF_ROWS = P // 2
 HALF_PACK = HALF_ROWS * PACK
 CHUNK_SIZES = (256, 256, 256, 256)
 CHUNKS = [(sum(CHUNK_SIZES[:c]), rows) for c, rows in enumerate(CHUNK_SIZES)]
-LATE_FROM = 768
+LATE_FROM = 256
 SPLITS = (-1.0 / 3.0, 1.0 / 3.0)
-UNITS_FIRST = 4
-UNITS_BETWEEN = {0: (3, 2), 1: (2, 1)}
+UNITS_FIRST = 2
+UNITS_BETWEEN = {0: (2, 2), 1: (3, 3)}
 QUANTISED_IN_ORDER = (2, 3, NB, 0, 1, 4, 5)
 
 TAIL_SCALE = 6.0 ** -0.5

from contextlib import ExitStack

import concourse.mybir as mybir
from concourse.masks import make_identity

F32 = mybir.dt.float32
BF16 = mybir.dt.bfloat16
U32 = mybir.dt.uint32
U8 = mybir.dt.uint8
I32 = mybir.dt.int32
FP8X4 = mybir.dt.float8_e4m3fn_x4
ALU = mybir.AluOpType
ACT = mybir.ActivationFunctionType

P = 128
PACK = 4
TOKENS = 1024
FEATURES = 512
OUTPUTS = 512
NB = 6
SLOTS = NB + 1
HALF = FEATURES // 2
HALF_ROWS = P // 2
HALF_PACK = HALF_ROWS * PACK
CHUNK_SIZES = (256, 256, 256, 256)
CHUNKS = [(sum(CHUNK_SIZES[:c]), rows) for c, rows in enumerate(CHUNK_SIZES)]
LATE_FROM = 256
SPLITS = (-1.0 / 3.0, 1.0 / 3.0)
UNITS_FIRST = 2
UNITS_BETWEEN = {0: (2, 2), 1: (3, 3)}
QUANTISED_IN_ORDER = (2, 3, NB, 0, 1, 4, 5)

TAIL_SCALE = 6.0 ** -0.5
RHO = (4.0 ** (1.0 / 3.0) + 16.0 ** (1.0 / 3.0) - 2.0) / 3.0
ALPHA = 1.0 + RHO / 2.0
BETA = RHO * (2.0 + RHO) - ALPHA * ALPHA
CORE_SCALE = 0.5 ** 0.5
assert all(
    abs((d + RHO) * ((d - ALPHA) ** 2 + BETA) / 2.0 - (2.0 / 3.0 - d * d + d ** 3 / 2.0)) < 1e-14
    for d in (0.0, 0.25, 0.5, 1.0, 2.0)
)

FLOPS = 2 * TOKENS * FEATURES * OUTPUTS * SLOTS


def turn_half_rows(nc, out, half_rows, ident):
    for e in range(2):
        nc.tensor.transpose(
            out.rearrange("p (r e u) -> p e r u", e=2, u=2)[:, e],
            half_rows[:, e * P : (e + 1) * P],
            ident,
        )


def tile_kanoriginal_kernel(
    tc, x, coef, scale_base_words, scale_base_scales, scale_sp, bias, out
):
    nc = tc.nc
    x_rows = x.flatten_outer_dims()
    out_rows = out.flatten_outer_dims()

    with ExitStack() as ctx:
        keep = ctx.enter_context(tc.tile_pool(name="keep", bufs=1))
        scalar_out = ctx.enter_context(tc.tile_pool(name="scalar_out", bufs=2))
        vector_own = ctx.enter_context(tc.tile_pool(name="vector_own", bufs=1))
        vector_out = ctx.enter_context(tc.tile_pool(name="vector_out", bufs=2))
        psum = ctx.enter_context(tc.psum_pool(name="psum", bufs=5))

        ctx.enter_context(tc.manual_schedule())

        x_sb = keep.tile([P, TOKENS // P, FEATURES], BF16)
        x_half_sb = keep.tile([P, TOKENS // HALF_ROWS, HALF], BF16)
        sp_sb = keep.tile([P, OUTPUTS // HALF_ROWS, HALF], BF16)
        coef_sb = keep.tile([P, OUTPUTS // HALF_ROWS, HALF * NB], BF16)
        coef_rows = coef.rearrange("o i b -> o (i b)")

        def load_half_rows(out, rows):
            nc.sync.dma_start(
                out=out, in_=rows.rearrange("(a r) (u i) -> (r u) a i", r=HALF_ROWS, u=2)
            )

        def load_x(first, rows):
            nc.sync.dma_start(
                out=x_sb[:, first // P : (first + rows) // P, :],
                in_=x_rows[first : first + rows, :].rearrange("(a r) i -> r a i", r=P),
            )

        def load_x_halves(first, rows):
            load_half_rows(
                x_half_sb[:, first // HALF_ROWS : (first + rows) // HALF_ROWS, :],
                x_rows[first : first + rows, :],
            )

        def load_sp(first, rows):
            load_half_rows(
                sp_sb[:, first // HALF_ROWS : (first + rows) // HALF_ROWS, :],
                scale_sp[first : first + rows, :],
            )

        def load_coef(first, rows):
            load_half_rows(
                coef_sb[:, first // HALF_ROWS : (first + rows) // HALF_ROWS, :],
                coef_rows[first : first + rows, :],
            )

        load_x_halves(*CHUNKS[0])
        load_sp(0, P)
        load_coef(0, HALF_ROWS)
        load_coef(HALF_ROWS, HALF_ROWS)
        load_x(*CHUNKS[0])
        load_sp(P, OUTPUTS - P)
        load_x_halves(*CHUNKS[1])
        load_coef(P, P)
        load_x(*CHUNKS[1])
        for a in range(2, OUTPUTS // P):
            load_coef(a * P, P)
        for chunk in CHUNKS[2:]:
            load_x_halves(*chunk)
            load_x(*chunk)
        w_codes = keep.tile([P, SLOTS, OUTPUTS], U32, align_bytes=64)
        w_planes = keep.tile([P, SLOTS, OUTPUTS], U8, align_bytes=64)
        nc.sync.dma_start(
            out=w_codes[:, NB, :].bitcast(I32),
            in_=scale_base_words.rearrange("g p n t -> (g p) (n t)").bitcast(I32),
        )
        nc.vector.memset(w_planes[:, NB, :].bitcast(I32), 0)
        base_scale_rows = scale_base_scales.rearrange("g q n -> (g q) n")
        for quadrant in range(4):
            nc.sync.dma_start(
                out=w_planes[32 * quadrant : 32 * quadrant + 4, NB, :].bitcast(I32),
                in_=base_scale_rows[4 * quadrant : 4 * quadrant + 4, :].bitcast(I32),
            )
        bias_all = keep.tile([P, OUTPUTS], BF16)
        nc.sync.dma_start(out=bias_all, in_=bias.partition_broadcast(P))

        ident_bf = keep.tile([P, P], BF16)
        make_identity(nc, ident_bf)
        ident = keep.tile([P, P], F32)
        make_identity(nc, ident)
        one = keep.tile([P, 1], F32)
        nc.vector.memset(one, 1.0)

        warm = keep.tile([P, 1], F32)
        nc.scalar.activation(out=warm, in_=one, func=ACT.Silu)

        def bias_column(name, value):
            column = keep.tile([P, 1], F32, name=name)
            nc.vector.tensor_scalar(
                out=column, in0=one, scalar1=value, scalar2=None, op0=ALU.mult
            )
            return column

        plus_half = bias_column("plus_half", 0.5)
        minus_half = bias_column("minus_half", -0.5)
        minus_one = bias_column("minus_one", -1.0)
        minus_two = bias_column("minus_two", -2.0)
        split_columns = [
            bias_column("split_%d" % i, -split) for i, split in enumerate(SPLITS)
        ]
        tail_bias = bias_column("tail_bias", -2.0 * TAIL_SCALE)
        line_bias_even = bias_column("line_bias_even", -(1.0 + RHO))
        line_bias_odd = bias_column("line_bias_odd", -RHO)
        quad_bias_even = bias_column("quad_bias_even", -(1.0 - ALPHA) * CORE_SCALE)
        quad_bias_odd = bias_column("quad_bias_odd", -ALPHA * CORE_SCALE)

        x_t = keep.tile([P, TOKENS * PACK], BF16)

        def turn_x(first, rows):
            bank = psum.tile([P, rows * PACK], BF16, tag="x", bufs=2)
            for a in range(rows // HALF_ROWS):
                turn_half_rows(
                    nc,
                    bank[:, a * HALF_PACK : (a + 1) * HALF_PACK],
                    x_half_sb[:, first // HALF_ROWS + a, :],
                    ident_bf,
                )
            return bank

        def turn_x_words(first, rows):
            bank = psum.tile([P, 2, rows], F32, tag="words", bufs=1)
            for a in range(rows // P):
                words = x_sb[:, first // P + a, :].bitcast(F32)
                for h in range(2):
                    nc.tensor.transpose(bank[:, h, a * P : (a + 1) * P], words[:, h::2], ident)
            return bank

        def scalar_part(first, rows, bank, words_bank):
            width = rows * PACK
            away = scalar_out.tile([P, 4, width], F32)
            nc.scalar.activation(
                out=away[:, 2, :], in_=bank, func=ACT.Abs, bias=plus_half, scale=1.5
            )
            nc.scalar.activation(
                out=away[:, 3, :], in_=bank, func=ACT.Abs, bias=minus_half, scale=1.5
            )
            x_c = x_t[:, first * PACK : first * PACK + width]
            if first < LATE_FROM:
                nc.scalar.copy(out=x_c, in_=bank)
            tail_squares = scalar_out.tile([P, 4, width], F32)
            nc.scalar.activation(
                out=tail_squares[:, 2:4, :], in_=away[:, 2:4, :], func=ACT.Square,
                bias=tail_bias, scale=TAIL_SCALE,
            )
            for i in range(2):
                nc.scalar.activation(
                    out=away[:, i, :], in_=away[:, 2 + i, :], func=ACT.Abs, bias=minus_two
                )
            to_odd = scalar_out.tile([P, width], F32)
            nc.scalar.activation(out=to_odd, in_=away[:, 0, :], func=ACT.Abs, bias=minus_one)
            nc.scalar.activation(
                out=tail_squares[:, 0:2, :], in_=away[:, 0:2, :], func=ACT.Square,
                bias=tail_bias, scale=TAIL_SCALE,
            )
            line = scalar_out.tile([P, 2, width], F32, bufs=1)
            quad = scalar_out.tile([P, 2, width], F32, bufs=1)
            nc.scalar.activation(
                out=line[:, 0, :], in_=to_odd, func=ACT.Identity, bias=line_bias_even
            )
            nc.scalar.activation(
                out=line[:, 1, :], in_=to_odd, func=ACT.Identity, bias=line_bias_odd, scale=-1.0
            )
            nc.scalar.activation(
                out=quad[:, 0, :], in_=to_odd, func=ACT.Square,
                bias=quad_bias_even, scale=CORE_SCALE,
            )
            nc.scalar.activation(
                out=quad[:, 1, :], in_=to_odd, func=ACT.Square,
                bias=quad_bias_odd, scale=CORE_SCALE,
            )
            silu = scalar_out.tile([P, width], BF16, align_bytes=64)
            nc.scalar.activation(
                out=silu.rearrange("p (r h e) -> p r h e", h=2, e=2),
                in_=words_bank.bitcast(BF16).rearrange("p h (r e) -> p r h e", e=2),
                func=ACT.Silu,
            )
            side = None
            if first >= LATE_FROM:
                side = scalar_out.tile([P, 2, width], BF16)
                for i, column in enumerate(split_columns):
                    nc.scalar.activation(out=side[:, i, :], in_=bank, func=ACT.Sign, bias=column)
            return silu, away, tail_squares, line, quad, side

        units = [(a, h) for a in range(OUTPUTS // P) for h in range(NB // 2)]
        waiting = []

        def next_unit():
            if units:
                a, h = units.pop(0)
                waiting.append(weight_piece(a, h))
                if h == 0 and a + 1 < OUTPUTS // P:
                    turn_sp(a + 1)
            if len(waiting) > 1 or (waiting and not units):
                quantise_piece(*waiting.pop(0))

        def vector_part(
            first, rows, units_between, unfinished, silu, away, tail_squares, line, quad, side
        ):
            width = rows * PACK
            x_c = x_t[:, first * PACK : first * PACK + width]
            pairs, singles = slice(0, 2), slice(2, 4)

            def make_side(side, i):
                nc.vector.tensor_scalar(
                    out=side[:, i, :], in0=x_c, scalar1=SPLITS[i], scalar2=0.5,
                    op0=ALU.is_ge, op1=ALU.subtract,
                )

            codes = vector_out.tile([P, SLOTS, rows], U32, align_bytes=64)
            planes = vector_out.tile([P, SLOTS, rows], U8, align_bytes=64)

            def quantise(values, slots):
                nc.vector.quantize_mx(
                    out=codes[:, slots, :].rearrange("p s n -> p (s n)").bitcast(FP8X4),
                    scales=planes[:, slots, :].rearrange("p s n -> p (s n)"),
                    in_=values,
                )

            neg = vector_own.tile([P, 4, width], BF16)
            for kind, count in zip((singles, pairs), units_between):
                nc.vector.scalar_tensor_tensor(
                    out=neg[:, kind, :], in0=away[:, kind, :], scalar=2.0,
                    in1=tail_squares[:, kind, :], op0=ALU.subtract, op1=ALU.mult,
                )
                for n in range(count):
                    next_unit()
            side_scale = 1.0
            if side is None:
                side = vector_own.tile([P, 2, width], BF16)
                side_scale = 0.5
                make_side(side, 0)
            neg_core = vector_own.tile([P, 2, width], BF16)
            nc.vector.scalar_tensor_tensor(
                out=neg_core, in0=quad, scalar=BETA / 2.0, in1=line, op0=ALU.add, op1=ALU.mult
            )
            if side_scale == 0.5:
                make_side(side, 1)
            while unfinished:
                finish(*unfinished.pop(0))
            if not units:
                while waiting:
                    next_unit()
            for kind in (singles, pairs):
                nc.vector.tensor_tensor(
                    out=neg[:, kind, :], in0=neg[:, kind, :], in1=neg_core, op=ALU.max
                )
            basis = vector_own.tile([P, NB, width], BF16, align_bytes=64)
            both = neg[:, pairs, :]
            nc.vector.tensor_scalar(
                out=basis[:, 2:4, :], in0=neg[:, singles, :], scalar1=-1.0, scalar2=0.0,
                op0=ALU.mult, op1=ALU.max,
            )
            nc.vector.tensor_scalar(
                out=both, in0=both, scalar1=0.0, scalar2=None, op0=ALU.min
            )
            quantise(basis[:, 2:4, :].rearrange("p s m -> p (s m)"), slice(2, 4))
            nc.vector.tensor_tensor(out=both, in0=both, in1=side, op=ALU.mult)
            quantise(silu, slice(NB, SLOTS))
            for low, sign in ((0, 1.0), (4, -1.0)):
                nc.vector.tensor_scalar(
                    out=basis[:, low : low + 2, :], in0=both, scalar1=sign / side_scale,
                    scalar2=0.0, op0=ALU.mult, op1=ALU.max,
                )
            quantise(basis[:, 0:2, :].rearrange("p s m -> p (s m)"), slice(0, 2))
            quantise(basis[:, 4:6, :].rearrange("p s m -> p (s m)"), slice(4, 6))
            return codes, planes

        def quantise_piece(piece, a, h):
            for e in range(2):
                nc.vector.quantize_mx(
                    out=w_codes[:, 2 * h + e, a * P : (a + 1) * P].bitcast(FP8X4),
                    scales=w_planes[:, 2 * h + e, a * P : (a + 1) * P],
                    in_=piece[:, e, :],
                )

        sp_t = keep.tile([P, OUTPUTS * PACK], BF16)

        def turn_sp(a):
            bank = psum.tile([P, P * PACK], BF16, tag="bank")
            for half in range(2):
                turn_half_rows(
                    nc,
                    bank[:, half * HALF_PACK : (half + 1) * HALF_PACK],
                    sp_sb[:, 2 * a + half, :],
                    ident_bf,
                )
            nc.vector.tensor_copy(out=sp_t[:, a * P * PACK : (a + 1) * P * PACK], in_=bank)

        def weight_piece(a, h):
            bank = psum.tile([P, 2, P * PACK], BF16, tag="bank")
            for half in range(2):
                for b in range(2):
                    turn_half_rows(
                        nc,
                        bank[:, b, half * HALF_PACK : (half + 1) * HALF_PACK],
                        coef_sb[:, 2 * a + half, :].rearrange("k (i b) -> k b i", b=NB)[
                            :, 2 * h + b, :
                        ],
                        ident_bf,
                    )
            piece = vector_own.tile([P, 2, P * PACK], BF16, bufs=3, align_bytes=64)
            nc.vector.tensor_tensor(
                out=piece,
                in0=bank,
                in1=sp_t[:, a * P * PACK : (a + 1) * P * PACK]
                .unsqueeze(1)
                .to_broadcast([P, 2, P * PACK]),
                op=ALU.mult,
            )
            return piece, a, h

        def multiply(rows, codes, planes, last_chunk):
            halves = [slice(0, OUTPUTS // 2), slice(OUTPUTS // 2, OUTPUTS)]
            columns = halves if last_chunk else [slice(0, OUTPUTS)]
            parts = [(j, cols) for j in range(rows // P) for cols in columns]
            sums = []
            for j, cols in parts:
                total = psum.tile([P, OUTPUTS], F32, tag="bank", name="sum")
                sums.append((j * P, cols, total[:, cols]))
            early, late = QUANTISED_IN_ORDER[:-2], QUANTISED_IN_ORDER[-2:]
            passes = [(slot, n) for slot in early for n in range(len(parts))]
            passes += [(slot, n) for n in range(len(parts)) for slot in late]
            for slot, n in passes:
                j, cols = parts[n]
                nc.tensor.matmul_mx(
                    out=sums[n][2],
                    lhsT=codes[:, slot, j * P : (j + 1) * P].bitcast(FP8X4),
                    lhsT_scale=planes[:, slot, j * P : (j + 1) * P],
                    rhs=w_codes[:, slot, cols].bitcast(FP8X4),
                    rhs_scale=w_planes[:, slot, cols],
                    start=(slot == QUANTISED_IN_ORDER[0]),
                    stop=(slot == QUANTISED_IN_ORDER[-1]),
                )
            return sums

        def finish(first, sums):
            for offset, cols, total in sums:
                row = first + offset
                result = vector_out.tile([P, OUTPUTS], F32, bufs=4)
                nc.vector.tensor_tensor(
                    out=result[:, cols], in0=total, in1=bias_all[:, cols], op=ALU.add
                )
                nc.sync.dma_start(out=out_rows[row : row + P, cols], in_=result[:, cols])

        bank = turn_x(*CHUNKS[0])
        turn_sp(0)
        for n in range(UNITS_FIRST):
            next_unit()
        made = scalar_part(*CHUNKS[0], bank, turn_x_words(*CHUNKS[0]))
        bank = turn_x(*CHUNKS[1])
        quantised = []
        unfinished = []
        for c, (first, rows) in enumerate(CHUNKS):
            codes, planes = vector_part(
                first, rows, UNITS_BETWEEN.get(c, (0, 0)), unfinished, *made
            )
            quantised.append((first, rows, codes, planes))
            if c + 1 < len(CHUNKS):
                made = scalar_part(*CHUNKS[c + 1], bank, turn_x_words(*CHUNKS[c + 1]))
            if c + 2 < len(CHUNKS):
                bank = turn_x(*CHUNKS[c + 2])
            if c > 0:
                while quantised:
                    first, rows, codes, planes = quantised.pop(0)
                    unfinished.append((first, multiply(rows, codes, planes, c + 1 == len(CHUNKS))))
        while unfinished:
            finish(*unfinished.pop(0))
